import numpy as np
import ml_dtypes


def mxq(x, axis, fmt="e4m3"):
    dtype, down = {"e4m3": (ml_dtypes.float8_e4m3fn, 7), "e5m2": (ml_dtypes.float8_e5m2, 14)}[fmt]
    v = np.moveaxis(np.asarray(x, np.float32).astype(ml_dtypes.bfloat16).astype(np.float64), axis, -1)
    blocks = v.reshape(v.shape[:-1] + (-1, 32))
    amax = np.abs(blocks).max(-1, keepdims=True)
    byte = np.maximum(np.where(amax > 0, np.frexp(amax)[1] - 1 + 127, 0) - down, 1)
    scale = np.exp2(byte - 127.0)
    codes = (blocks / scale).astype(np.float32).astype(dtype).astype(np.float64)
    return np.moveaxis((codes * scale).reshape(v.shape), -1, axis)


WIDE = False


def mx_kscale(k):
    if not WIDE:
        return np.ones(k)
    levels = np.array([10, -10, 5, -5, 0])
    if k % 512:
        return np.exp2(np.random.permutation(np.resize(levels, k // 32))).repeat(32)
    a = np.empty((k // 512, 16))
    for p in range(k // 512):
        a[p, :8] = np.random.permutation(np.resize(levels, 8))
        for g in range(8):
            far = levels[np.abs(levels - a[p, g]) >= 10]
            a[p, g + 8] = far[np.random.randint(len(far))]
    return np.exp2(a.ravel()).repeat(32)


BF16 = ml_dtypes.bfloat16


def bf(x):
    return np.asarray(x, np.float32).astype(BF16)


def f64(x):
    return np.asarray(x).astype(np.float64)


B, D_IN, D_H, C = 8192, 512, 512, 128
TAU, T1, T2 = 0.5, 3, 3
G, GB = 3.0, 3.0


def inv_apprx(v, t, m):
    a = 2.0 - (2.0 / m) * v
    b = 1.0 - (2.0 / m) * v
    for _ in range(t):
        b = b * b
        a = a * (1.0 + b)
    return (2.0 / m) * a


def comp_max_tau(p, tau, t1, t2):
    res = np.concatenate([p, np.full((p.shape[0], 1), tau)], axis=1)
    for i in range(t1):
        res = res * res
        sum_res = res.sum(axis=1)
        m = (2.0 + tau * tau) if i == 0 else 2.0
        res = res * inv_apprx(sum_res, t2, m)[:, None]
    return res[:, -1]


def softmax(z):
    e = np.exp(z - z.max(-1, keepdims=True))
    return e / e.sum(-1, keepdims=True)


def mlp(xq, W1, b1, W2, b2):
    h = np.maximum((xq @ mxq(f64(W1), 0, "e4m3")) + f64(b1), 0.0)
    return softmax((mxq(h, 1, "e4m3") @ mxq(f64(W2), 0, "e4m3")) + f64(b2))


def draw0():
    s, t = mx_kscale(D_IN), mx_kscale(D_H)
    return {"x": bf(np.random.standard_normal((B, D_IN)) * s),
            "W1o": bf(np.random.standard_normal((D_IN, D_H)) / np.sqrt(D_IN) / s[:, None] * t),
            "b1o": bf(np.random.standard_normal(D_H) * 0.2 * t),
            "W2o": bf(np.random.standard_normal((D_H, C)) * G / np.sqrt(D_H) / t[:, None]),
            "b2o": bf(np.random.standard_normal(C) * GB),
            "W1f": bf(np.random.standard_normal((D_IN, D_H)) / np.sqrt(D_IN) / s[:, None] * t),
            "b1f": bf(np.random.standard_normal(D_H) * 0.2 * t),
            "W2f": bf(np.random.standard_normal((D_H, C)) * G / np.sqrt(D_H) / t[:, None]),
            "b2f": bf(np.random.standard_normal(C) * GB)}


def core(x, W1o, b1o, W2o, b2o, W1f, b1f, W2f, b2f):
    xq = mxq(f64(x), 1, "e4m3")
    x1 = mlp(xq, W1o, b1o, W2o, b2o)
    x2 = mlp(xq, W1f, b1f, W2f, b2f)
    cond_in = comp_max_tau(x1, TAU, T1, T2)
    return x1 * (1.0 - cond_in[:, None]) + x2 * cond_in[:, None]


def e4m3fn_bytes(y):
    return np.clip(np.asarray(y, np.float64), -448.0, 448.0).astype(np.float32).astype(ml_dtypes.float8_e4m3fn).view(np.uint8)


def e4m3fn_values(b):
    return np.asarray(b, np.uint8).view(ml_dtypes.float8_e4m3fn).astype(np.float64)


def setup_inputs():
    d = draw0()
    x0 = np.asarray(d['x']).astype(np.float64)
    s = (np.max(np.abs(x0), axis=(0,), keepdims=True) / 448.0).astype(np.float32)
    out = {}
    for k, v in d.items():
        if k == 'x':
            out['x_bytes'] = e4m3fn_bytes(x0 / s.astype(np.float64))
            out['x_scale'] = s
        else:
            out[k] = v
    return out


def reference(x_bytes, x_scale, W1o, b1o, W2o, b2o, W1f, b1f, W2f, b2f):
    return core(e4m3fn_values(x_bytes) * x_scale.astype(np.float64), W1o, b1o, W2o, b2o, W1f, b1f, W2f, b2f)

@@ -1,0 +1,374 @@
+from contextlib import ExitStack
+
+import concourse.mybir as mybir
+from concourse.masks import make_identity
+
+B, D_IN, D_H, C = 8192, 512, 512, 128
+FLOPS = 2 * (2 * B * D_IN * D_H + 2 * B * D_H * C)
+
+TAU = 0.5
+
+F32 = mybir.dt.float32
+BF16 = mybir.dt.bfloat16
+U32 = mybir.dt.uint32
+U8 = mybir.dt.uint8
+FP8 = mybir.dt.float8_e4m3fn
+FP8X4 = mybir.dt.float8_e4m3fn_x4
+ACT = mybir.ActivationFunctionType
+ALU = mybir.AluOpType
+AX = mybir.AxisListType
+
+P = 128
+UNIT = 512
+BLK = UNIT // P
+N_UNITS = B // UNIT
+GATE_UNITS = 8
+
+
+def tile_combnethe_pa_t_kernel(tc, x_bytes, x_scale, W1o, b1o, W2o, b2o, W1f, b1f, W2f, b2f, out):
+    nc = tc.nc
+    x_rows = x_bytes.rearrange("(i p b) k -> i p b k", p=P, b=BLK)
+    out_rows = out.rearrange("(i p b) c -> i p b c", p=P, b=BLK)
+    w1_in, b1_in, w2_in, b2_in = (W1o, W1f), (b1o, b1f), (W2o, W2f), (b2o, b2f)
+
+    with ExitStack() as ctx:
+        keep = ctx.enter_context(tc.tile_pool(name="keep", bufs=1))
+        work = ctx.enter_context(tc.tile_pool(name="work", bufs=3))
+        psum = ctx.enter_context(tc.psum_pool(name="psum", bufs=2))
+        ctx.enter_context(tc.manual_schedule())
+
+        ident = keep.tile([P, P], F32, name="ident")
+        scale = keep.tile([P, 2, D_IN], F32, name="scale")
+        w1_codes = [keep.tile([P, D_H], U32, name="w1c%d" % n, align_bytes=64) for n in range(2)]
+        w1_scales = [keep.tile([P, D_H], U8, name="w1s%d" % n, align_bytes=64) for n in range(2)]
+        w2_codes = keep.tile([P, 2 * C], U32, name="w2c", align_bytes=64)
+        w2_scales = keep.tile([P, 2 * C], U8, name="w2s", align_bytes=64)
+        b1 = [keep.tile([P, 4], BF16, name="b1_%d" % n) for n in range(2)]
+        b2 = [keep.tile([P, 1], BF16, name="b2_%d" % n) for n in range(2)]
+        b2n = [keep.tile([P, 1], F32, name="b2n_%d" % n) for n in range(2)]
+        warm = keep.tile([P, 1], F32, name="warm")
+
+        xb, xs, xt, xg, xq = {}, {}, {}, {}, {}
+        ps1, hp, hg, hq, ps2, zt, zl, nm, ez, e2s, e4, t1 = {}, {}, {}, {}, {}, {}, {}, {}, {}, {}, {}, {}
+        rz2, beta, zsum2 = {}, {}, {}
+
+        n_gate = N_UNITS // GATE_UNITS
+        gcols = GATE_UNITS * BLK
+        zsum = [keep.tile([P, gcols], F32, name="zsum%d" % g) for g in range(n_gate)]
+        s2 = [keep.tile([P, gcols], F32, name="s2_%d" % g) for g in range(n_gate)]
+        stats = [keep.tile([P, gcols, 6], F32, name="stats%d" % g) for g in range(n_gate)]
+        alpha = [keep.tile([P, gcols], F32, name="alpha%d" % g) for g in range(n_gate)]
+        cond = [keep.tile([P, gcols], F32, name="cond%d" % g) for g in range(n_gate)]
+
+        def col(i, b):
+            return i // GATE_UNITS, (i % GATE_UNITS) * BLK + b
+
+        def load(i):
+            t = work.tile([P, BLK, D_IN], U8, name="xb", bufs=8)
+            nc.sync.dma_start(out=t[:], in_=x_rows[i])
+            xb[i] = t
+
+        def widen(i, h):
+            t = work.tile([P, 2, D_IN], BF16, name="xs", bufs=4, align_bytes=64)
+            nc.vector.tensor_tensor(
+                out=t[:].rearrange("p b k -> p (b k)"),
+                in0=xb[i][:, 2 * h : 2 * h + 2, :].rearrange("p b k -> p (b k)").bitcast(FP8),
+                in1=scale[:].rearrange("p b k -> p (b k)"), op=ALU.mult)
+            xs[i, h] = t
+
+        def turn(i, h):
+            t = psum.tile([P, 2, 2, P], F32, name="xt", bufs=2)
+            words = xs[i, h][:].rearrange("p b k -> p (b k)").bitcast(F32)
+            for b in range(2):
+                for u in range(2):
+                    nc.tensor.transpose(t[:, b, u, :], words[:, 256 * b + u : 256 * (b + 1) : 2], ident[:])
+            xt[i, h] = t
+
+        def leave(i, h):
+            if h == 0:
+                xg[i] = work.tile([P, UNIT, 4], BF16, name="xg", bufs=3, align_bytes=64)
+            words = xg[i][:].rearrange("p n j -> p (n j)").bitcast(F32).rearrange("p (b r u) -> p b r u", b=BLK, u=2)
+            nc.scalar.copy(out=words[:, 2 * h : 2 * h + 2], in_=xt[i, h][:].rearrange("p b u r -> p b r u"))
+
+        def quant_x(i):
+            codes = work.tile([P, UNIT], U32, name="xq", bufs=N_UNITS, align_bytes=64)
+            scales = work.tile([P, UNIT], U8, name="xqs", bufs=N_UNITS, align_bytes=64)
+            nc.vector.quantize_mx(out=codes[:].bitcast(FP8X4), scales=scales[:], in_=xg[i][:].rearrange("p n j -> p (n j)"))
+            xq[i] = (codes, scales)
+
+        def mm1(n, i):
+            codes, scales = xq[i]
+            for t in range(4):
+                acc = psum.tile([P, UNIT], F32, name="ps1", bufs=4)
+                m = slice(P * t, P * (t + 1))
+                nc.tensor.matmul_mx(out=acc[:], lhsT=w1_codes[n][:, m].bitcast(FP8X4), lhsT_scale=w1_scales[n][:, m],
+                                    rhs=codes[:].bitcast(FP8X4), rhs_scale=scales[:], start=True, stop=True)
+                ps1[n, i, t] = acc
+
+        def relu(n, i):
+            hp[n, i] = work.tile([P, 4, UNIT], BF16, name="hp", bufs=3, align_bytes=64)
+            for t in range(4):
+                nc.scalar.activation(hp[n, i][:, t, :], ps1[n, i, t][:], ACT.Relu, bias=b1[n][:, t : t + 1])
+
+        def weave(n, i):
+            hg[n, i] = work.tile([P, UNIT, 4], BF16, name="hg", bufs=3, align_bytes=64)
+            nc.vector.tensor_copy(out=hg[n, i][:].rearrange("p (c i) t -> p c t i", i=4),
+                                  in_=hp[n, i][:].rearrange("p t (c i) -> p c t i", i=4))
+
+        def quant_h(n, i):
+            codes = work.tile([P, UNIT], U32, name="hq", bufs=3, align_bytes=64)
+            scales = work.tile([P, UNIT], U8, name="hqs", bufs=3, align_bytes=64)
+            nc.vector.quantize_mx(out=codes[:].bitcast(FP8X4), scales=scales[:], in_=hg[n, i][:].rearrange("p n j -> p (n j)"))
+            hq[n, i] = (codes, scales)
+
+        def mm2(n, i):
+            codes, scales = hq[n, i]
+            acc = psum.tile([P, UNIT], F32, name="ps2", bufs=1)
+            w = slice(C * n, C * (n + 1))
+            nc.tensor.matmul_mx(out=acc[:], lhsT=w2_codes[:, w].bitcast(FP8X4), lhsT_scale=w2_scales[:, w],
+                                rhs=codes[:].bitcast(FP8X4), rhs_scale=scales[:], start=True, stop=True)
+            ps2[n, i] = acc
+
+        def logits(n, i):
+            zl[n, i] = work.tile([P, UNIT], F32, name="zl", bufs=2)
+            nc.scalar.activation(zl[n, i][:], ps2[n, i][:], ACT.Identity, bias=b2n[n][:], scale=-1.0)
+
+        def turn_logits(n, i):
+            zt[n, i] = psum.tile([P, BLK, C], F32, name="zt", bufs=1)
+            for b in range(BLK):
+                nc.tensor.transpose(zt[n, i][:, b, :], zl[n, i][:, P * b : P * (b + 1)], ident[:])
+
+        def rowmin(n, i):
+            nm[n, i] = work.tile([P, BLK], F32, name="nm", bufs=4)
+            nc.vector.tensor_reduce(out=nm[n, i][:], in_=zt[n, i][:], axis=AX.X, op=ALU.min)
+
+        def exps(n, i):
+            ez[n, i] = work.tile([P, BLK, C], F32, name="ez%d" % n, bufs=N_UNITS if n == 0 else 6)
+            if n == 1:
+                zsum2[i] = work.tile([P, BLK], F32, name="zsum2", bufs=4)
+            for b in range(BLK):
+                g, c = col(i, b)
+                acc = zsum[g][:, c : c + 1] if n == 0 else zsum2[i][:, b : b + 1]
+                nc.scalar.activation(ez[n, i][:, b, :], zt[n, i][:, b, :], ACT.Exp, bias=nm[n, i][:, b : b + 1], scale=-1.0, accum_out=acc)
+
+        def powers(i):
+            e2 = work.tile([P, BLK, C], F32, name="e2", bufs=2)
+            for b in range(BLK):
+                g, c = col(i, b)
+                nc.scalar.activation(e2[:, b, :], ez[0, i][:, b, :], ACT.Square, accum_out=s2[g][:, c : c + 1])
+            e2s[i] = e2
+
+        def fourth(i):
+            e4[i] = work.tile([P, BLK, C], F32, name="e4", bufs=3)
+            nc.scalar.activation(e4[i][:], e2s[i][:], ACT.Square)
+
+        def power_stats(i):
+            for b in range(BLK):
+                g, c = col(i, b)
+                nc.vector.bn_stats(out=stats[g][:, c, :], in_=e4[i][:, b, :])
+
+        def gate(g):
+            names = {}
+
+            def tmp(key):
+                names[key] = work.tile([P, gcols], F32, name="g_" + key, bufs=1)
+                return names[key]
+
+            def get(key):
+                return names[key] if isinstance(key, str) else key
+
+            ops = []
+
+            def mul(dst, a, b):
+                ops.append(lambda: nc.gpsimd.tensor_tensor(out=(tmp(dst) if isinstance(dst, str) else dst)[:], in0=get(a)[:], in1=get(b)[:], op=ALU.mult))
+
+            def stat(k):
+                return stats[g][:, :, k]
+
+            def tt(dst, a, b, op):
+                ops.append(lambda: nc.gpsimd.tensor_tensor(out=tmp(dst)[:], in0=get(a)[:] if isinstance(a, str) else a, in1=get(b)[:] if isinstance(b, str) else b, op=op))
+
+            def lin(dst, a, m, c):
+                ops.append(lambda: nc.gpsimd.tensor_scalar(out=tmp(dst)[:], in0=get(a)[:], scalar1=m, scalar2=c, op0=ALU.mult, op1=ALU.add))
+
+            def inv(r, v, vm, vc, two_over_m):
+                lin("y" + r, v, vm, vc)
+                lin("a" + r, "y" + r, two_over_m, two_over_m)
+                prev, a = "y" + r, "a" + r
+                for s in ("2", "4", "8"):
+                    mul("y" + s + r, prev, prev)
+                    lin("c" + s + r, "y" + s + r, 1.0, 1.0)
+                    mul("a" + s + r, a, "c" + s + r)
+                    prev, a = "y" + s + r, "a" + s + r
+                return a
+
+            t2, t4, t8 = TAU**2, TAU**4, TAU**8
+            m0 = 2.0 + t2
+            ops.append(lambda: nc.vector.reciprocal(out=tmp("r")[:], in_=zsum[g][:]))
+            mul("q", "r", "r")
+            mul("u1", s2[g], "q")
+            k1 = inv("i", "u1", -2.0 / m0, 1.0 - 2.0 / m0 * t2, 2.0 / m0)
+            mul("k1s", k1, k1)
+            mul("q2", "q", "q")
+            half = C / 2.0
+            tt("ms", stat(1), stat(4), ALU.add)
+            lin("s4", "ms", half, 0.0)
+            tt("me2", stat(1), stat(1), ALU.mult)
+            tt("mo2", stat(4), stat(4), ALU.mult)
+            tt("m2", "me2", "mo2", ALU.add)
+            lin("m2h", "m2", half, 0.0)
+            tt("vs", stat(2), stat(5), ALU.add)
+            tt("s8", "vs", "m2h", ALU.add)
+            mul("u2", "s4", "q2")
+            lin("w2", "u2", 1.0, t4)
+            mul("v2", "w2", "k1s")
+            i2 = inv("j", "v2", -1.0, 1.0, 1.0)
+            mul("k2", "k1s", i2)
+            mul("k2s", "k2", "k2")
+            mul("q4", "q2", "q2")
+            mul("u3", "s8", "q4")
+            lin("w3", "u3", 1.0, t8)
+            mul("v3", "w3", "k2s")
+            i3 = inv("k", "v3", -1.0, 1.0, 1.0)
+            lin("k2t", "k2s", t8, 0.0)
+            mul(cond[g], "k2t", i3)
+            lin("d", cond[g], -1.0, 1.0)
+            mul(alpha[g], "d", "r")
+            return ops
+
+        def first_term(i):
+            t1[i] = work.tile([P, BLK, C], F32, name="t1", bufs=5)
+            for b in range(BLK):
+                g, c = col(i, b)
+                nc.gpsimd.tensor_scalar(out=t1[i][:, b, :], in0=ez[0, i][:, b, :], scalar1=alpha[g][:, c : c + 1], scalar2=0.0, op0=ALU.mult, op1=ALU.add)
+
+        def recip2(i):
+            rz2[i] = work.tile([P, BLK], F32, name="rz2", bufs=4)
+            nc.vector.reciprocal(out=rz2[i][:], in_=zsum2[i][:])
+            beta[i] = work.tile([P, BLK], F32, name="beta", bufs=4)
+            g, c = col(i, 0)
+            nc.gpsimd.tensor_tensor(out=beta[i][:], in0=rz2[i][:], in1=cond[g][:, c : c + BLK], op=ALU.mult)
+
+        def blend(i):
+            ob = work.tile([P, BLK, C], F32, name="ob", bufs=4)
+            for b in range(BLK):
+                nc.vector.scalar_tensor_tensor(out=ob[:, b, :], in0=ez[1, i][:, b, :], scalar=beta[i][:, b : b + 1], in1=t1[i][:, b, :],
+                                               op0=ALU.mult, op1=ALU.add)
+            nc.sync.dma_start(out=out_rows[i], in_=ob[:])
+
+        w_raw, w_grp = {}, {}
+
+        def load_w1(n):
+            w_raw[n] = keep.tile([P, 4, D_H], BF16, name="w1raw%d" % n)
+            nc.sync.dma_start(out=w_raw[n][:], in_=w1_in[n].rearrange("(p j) c -> p j c", j=4))
+
+        def group_w1(n, copy):
+            w_grp[n] = keep.tile([P, D_H, 4], BF16, name="w1grp%d" % n, align_bytes=64)
+            copy(out=w_grp[n][:].rearrange("p (t m) j -> p t m j", t=4), in_=w_raw[n][:].rearrange("p j (m t) -> p t m j", t=4))
+
+        def quant_w1(n):
+            nc.vector.quantize_mx(out=w1_codes[n][:].bitcast(FP8X4), scales=w1_scales[n][:], in_=w_grp[n][:].rearrange("p c j -> p (c j)"))
+
+        nc.vector.memset(warm[:], 0.0)
+        make_identity(nc, ident[:])
+        nc.sync.dma_start(out=scale[:, 0, :], in_=x_scale.rearrange("o k -> (o k)").partition_broadcast(P))
+        load(0)
+        load_w1(0)
+        load(1)
+        w2_raw = keep.tile([P, 2, 4, C], BF16, name="w2raw")
+        for n in range(2):
+            nc.sync.dma_start(out=w2_raw[:, n], in_=w2_in[n].rearrange("(p j) c -> p j c", j=4))
+        load(2)
+        load(3)
+        for n in range(2):
+            nc.scalar.dma_start(out=b1[n][:], in_=b1_in[n].rearrange("(p t) -> p t", t=4))
+        for n in range(2):
+            nc.scalar.dma_start(out=b2[n][:], in_=b2_in[n].rearrange("(c o) -> c o", o=1))
+        load_w1(1)
+        load(4)
+        load(5)
+        nc.scalar.activation(warm[:], warm[:], ACT.Exp)
+        group_w1(0, nc.scalar.copy)
+        nc.vector.tensor_copy(out=scale[:, 1, :], in_=scale[:, 0, :])
+        for h in range(2):
+            widen(0, h)
+            turn(0, h)
+            leave(0, h)
+        widen(1, 0)
+        turn(1, 0)
+        quant_w1(0)
+        widen(1, 1)
+        turn(1, 1)
+        quant_x(0)
+        mm1(0, 0)
+        for n in range(2):
+            nc.vector.tensor_scalar(out=b2n[n][:], in0=b2[n][:], scalar1=-1.0, scalar2=None, op0=ALU.mult)
+        for h in range(2):
+            leave(1, h)
+        w2_grp = keep.tile([P, 2, C, 4], BF16, name="w2grp", align_bytes=64)
+        for n in range(2):
+            nc.vector.tensor_copy(out=w2_grp[:, n], in_=w2_raw[:, n].rearrange("p j c -> p c j"))
+
+        items = [(0, i) for i in range(N_UNITS)] + [(1, i) for i in range(N_UNITS)]
+        n_items = len(items)
+        gate_ops = []
+        for q in range(n_items + 5):
+
+            def item(k):
+                return items[k] if 0 <= k < n_items else None
+
+            now, nxt, prev, prev2, prev3, prev4 = (item(q + d) for d in (0, 1, -1, -2, -3, -4))
+            if q + 6 < N_UNITS:
+                load(q + 6)
+            if now:
+                relu(*now)
+            if nxt and nxt[0] == 1:
+                mm1(*nxt)
+            if q + 2 < N_UNITS:
+                for h in range(2):
+                    widen(q + 2, h)
+                    turn(q + 2, h)
+            if prev3 and prev3[0] == 0:
+                power_stats(prev3[1])
+                if prev3[1] % GATE_UNITS == GATE_UNITS - 1:
+                    gate_ops += gate(prev3[1] // GATE_UNITS)
+            if prev3 and prev3[0] == 1:
+                recip2(prev3[1])
+            if prev2:
+                exps(*prev2)
+                if prev2[0] == 1:
+                    first_term(prev2[1])
+            if prev:
+                logits(*prev)
+                turn_logits(*prev)
+            if nxt and nxt[0] == 0:
+                quant_x(nxt[1])
+                mm1(*nxt)
+            if now:
+                weave(*now)
+            if q == 0:
+                nc.vector.quantize_mx(out=w2_codes[:].bitcast(FP8X4), scales=w2_scales[:], in_=w2_grp[:].rearrange("p n c j -> p (n c j)"))
+            if prev4 and prev4[0] == 1:
+                blend(prev4[1])
+            if now:
+                if now[0] == 0 and prev:
+                    rowmin(*prev)
+                quant_h(*now)
+                mm2(*now)
+            if prev and not (now and now[0] == 0):
+                rowmin(*prev)
+            if q == 6:
+                group_w1(1, nc.vector.tensor_copy)
+            if q == 7:
+                quant_w1(1)
+            if prev2 and prev2[0] == 0:
+                powers(prev2[1])
+            for op in gate_ops[:8]:
+                op()
+            gate_ops = gate_ops[8:]
+            if q + 2 < N_UNITS:
+                leave(q + 2, 0)
+            if prev2 and prev2[0] == 0:
+                fourth(prev2[1])
+            if q + 2 < N_UNITS:
+                leave(q + 2, 1)

@@ -22,7 +22,7 @@ P = 128
 UNIT = 512
 BLK = UNIT // P
 N_UNITS = B // UNIT
-GATE_UNITS = 8
+GATE_UNITS = 16
 
 
 def tile_combnethe_pa_t_kernel(tc, x_bytes, x_scale, W1o, b1o, W2o, b2o, W1f, b1f, W2f, b2f, out):
@@ -49,22 +49,18 @@ def tile_combnethe_pa_t_kernel(tc, x_bytes, x_scale, W1o, b1o, W2o, b2o, W1f, b1
         warm = keep.tile([P, 1], F32, name="warm")
 
         xb, xs, xt, xg, xq = {}, {}, {}, {}, {}
-        ps1, hp, hg, hq, ps2, zt, zl, nm, ez, e2s, e4, t1 = {}, {}, {}, {}, {}, {}, {}, {}, {}, {}, {}, {}
-        rz2, beta, zsum2 = {}, {}, {}
+        ps1, hp, hg, hq, ps2, zt, zl, nm, ez, e2s, e4 = {}, {}, {}, {}, {}, {}, {}, {}, {}, {}, {}
 
-        n_gate = N_UNITS // GATE_UNITS
-        gcols = GATE_UNITS * BLK
-        zsum = [keep.tile([P, gcols], F32, name="zsum%d" % g) for g in range(n_gate)]
-        s2 = [keep.tile([P, gcols], F32, name="s2_%d" % g) for g in range(n_gate)]
-        stats = [keep.tile([P, gcols, 6], F32, name="stats%d" % g) for g in range(n_gate)]
-        alpha = [keep.tile([P, gcols], F32, name="alpha%d" % g) for g in range(n_gate)]
-        cond = [keep.tile([P, gcols], F32, name="cond%d" % g) for g in range(n_gate)]
-
-        def col(i, b):
-            return i // GATE_UNITS, (i % GATE_UNITS) * BLK + b
+        cols = N_UNITS * BLK
+        zsum = keep.tile([P, cols], F32, name="zsum")
+        s2 = keep.tile([P, cols], F32, name="s2")
+        stats = keep.tile([P, cols // 2, 2, 3], F32, name="stats")
+        alpha = keep.tile([P, cols], F32, name="alpha")
+        cond = keep.tile([P, cols], F32, name="cond")
+        zsum2 = keep.tile([P, cols], F32, name="zsum2")
 
         def load(i):
-            t = work.tile([P, BLK, D_IN], U8, name="xb", bufs=8)
+            t = work.tile([P, BLK, D_IN], U8, name="xb", bufs=6)
             nc.sync.dma_start(out=t[:], in_=x_rows[i])
             xb[i] = t
 
@@ -143,19 +139,17 @@ def tile_combnethe_pa_t_kernel(tc, x_bytes, x_scale, W1o, b1o, W2o, b2o, W1f, b1
             nc.vector.tensor_reduce(out=nm[n, i][:], in_=zt[n, i][:], axis=AX.X, op=ALU.min)
 
         def exps(n, i):
-            ez[n, i] = work.tile([P, BLK, C], F32, name="ez%d" % n, bufs=N_UNITS if n == 0 else 6)
-            if n == 1:
-                zsum2[i] = work.tile([P, BLK], F32, name="zsum2", bufs=4)
+            ez[n, i] = work.tile([P, BLK, C], F32, name="ez%d" % n, bufs=N_UNITS if n == 0 else 9)
+            acc = zsum if n == 0 else zsum2
             for b in range(BLK):
-                g, c = col(i, b)
-                acc = zsum[g][:, c : c + 1] if n == 0 else zsum2[i][:, b : b + 1]
-                nc.scalar.activation(ez[n, i][:, b, :], zt[n, i][:, b, :], ACT.Exp, bias=nm[n, i][:, b : b + 1], scale=-1.0, accum_out=acc)
+                c = BLK * i + b
+                nc.scalar.activation(ez[n, i][:, b, :], zt[n, i][:, b, :], ACT.Exp, bias=nm[n, i][:, b : b + 1], scale=-1.0, accum_out=acc[:, c : c + 1])
 
         def powers(i):
             e2 = work.tile([P, BLK, C], F32, name="e2", bufs=2)
             for b in range(BLK):
-                g, c = col(i, b)
-                nc.scalar.activation(e2[:, b, :], ez[0, i][:, b, :], ACT.Square, accum_out=s2[g][:, c : c + 1])
+                c = BLK * i + b
+                nc.scalar.activation(e2[:, b, :], ez[0, i][:, b, :], ACT.Square, accum_out=s2[:, c : c + 1])
             e2s[i] = e2
 
         def fourth(i):
@@ -163,98 +157,93 @@ def tile_combnethe_pa_t_kernel(tc, x_bytes, x_scale, W1o, b1o, W2o, b2o, W1f, b1
             nc.scalar.activation(e4[i][:], e2s[i][:], ACT.Square)
 
         def power_stats(i):
-            for b in range(BLK):
-                g, c = col(i, b)
-                nc.vector.bn_stats(out=stats[g][:, c, :], in_=e4[i][:, b, :])
+            for h in range(2):
+                nc.vector.bn_stats(out=stats[:, 2 * i + h].rearrange("p b s -> p (b s)"), in_=e4[i][:, 2 * h : 2 * h + 2, :].rearrange("p b c -> p c b"))
 
-        def gate(g):
-            names = {}
-
-            def tmp(key):
-                names[key] = work.tile([P, gcols], F32, name="g_" + key, bufs=1)
-                return names[key]
-
-            def get(key):
-                return names[key] if isinstance(key, str) else key
-
+        def gate():
+            t = {}
             ops = []
+            per = stats[:].rearrange("p g b s -> p (g b) s")
+            mean, m2 = per[:, :, 1], per[:, :, 2]
+            t["z"], t["s2"], t["cond"], t["alpha"] = zsum, s2, cond, alpha
+
+            def new(key):
+                if key not in t:
+                    t[key] = work.tile([P, cols], F32, name="g_" + key, bufs=1)
+                return t[key][:]
+
+            def val(a):
+                return t[a][:] if isinstance(a, str) else a
+
+            def recip(dst, a):
+                ops.append(lambda: nc.vector.reciprocal(out=new(dst), in_=val(a)))
 
             def mul(dst, a, b):
-                ops.append(lambda: nc.gpsimd.tensor_tensor(out=(tmp(dst) if isinstance(dst, str) else dst)[:], in0=get(a)[:], in1=get(b)[:], op=ALU.mult))
-
-            def stat(k):
-                return stats[g][:, :, k]
-
-            def tt(dst, a, b, op):
-                ops.append(lambda: nc.gpsimd.tensor_tensor(out=tmp(dst)[:], in0=get(a)[:] if isinstance(a, str) else a, in1=get(b)[:] if isinstance(b, str) else b, op=op))
+                ops.append(lambda: nc.vector.tensor_tensor(out=new(dst), in0=val(a), in1=val(b), op=ALU.mult))
 
             def lin(dst, a, m, c):
-                ops.append(lambda: nc.gpsimd.tensor_scalar(out=tmp(dst)[:], in0=get(a)[:], scalar1=m, scalar2=c, op0=ALU.mult, op1=ALU.add))
+                ops.append(lambda: nc.vector.tensor_scalar(out=new(dst), in0=val(a), scalar1=m, scalar2=c, op0=ALU.mult, op1=ALU.add))
 
-            def inv(r, v, vm, vc, two_over_m):
+            def fma(dst, a, op0, s, op1, b):
+                ops.append(lambda: nc.vector.scalar_tensor_tensor(out=new(dst), in0=val(a), scalar=s, in1=val(b), op0=op0, op1=op1))
+
+            def inv(r, v, vm, vc, two_over_m, extra):
                 lin("y" + r, v, vm, vc)
-                lin("a" + r, "y" + r, two_over_m, two_over_m)
-                prev, a = "y" + r, "a" + r
-                for s in ("2", "4", "8"):
-                    mul("y" + s + r, prev, prev)
-                    lin("c" + s + r, "y" + s + r, 1.0, 1.0)
-                    mul("a" + s + r, a, "c" + s + r)
-                    prev, a = "y" + s + r, "a" + s + r
-                return a
+                lin("a" + r, v, vm * two_over_m, (vc + 1.0) * two_over_m)
+                mul("y2" + r, "y" + r, "y" + r)
+                for f in extra:
+                    f()
+                mul("y4" + r, "y2" + r, "y2" + r)
+                fma("b" + r, "y2" + r, ALU.add, 1.0, ALU.mult, "a" + r)
+                mul("y8" + r, "y4" + r, "y4" + r)
+                fma("c" + r, "y4" + r, ALU.add, 1.0, ALU.mult, "b" + r)
+                fma("d" + r, "y8" + r, ALU.add, 1.0, ALU.mult, "c" + r)
+                return "d" + r
 
+            n = float(C)
             t2, t4, t8 = TAU**2, TAU**4, TAU**8
             m0 = 2.0 + t2
-            ops.append(lambda: nc.vector.reciprocal(out=tmp("r")[:], in_=zsum[g][:]))
+            recip("r", "z")
+            mul("msq", mean, mean)
             mul("q", "r", "r")
-            mul("u1", s2[g], "q")
-            k1 = inv("i", "u1", -2.0 / m0, 1.0 - 2.0 / m0 * t2, 2.0 / m0)
-            mul("k1s", k1, k1)
+            fma("s8", "msq", ALU.mult, n, ALU.add, m2)
+            mul("u1", "s2", "q")
             mul("q2", "q", "q")
-            half = C / 2.0
-            tt("ms", stat(1), stat(4), ALU.add)
-            lin("s4", "ms", half, 0.0)
-            tt("me2", stat(1), stat(1), ALU.mult)
-            tt("mo2", stat(4), stat(4), ALU.mult)
-            tt("m2", "me2", "mo2", ALU.add)
-            lin("m2h", "m2", half, 0.0)
-            tt("vs", stat(2), stat(5), ALU.add)
-            tt("s8", "vs", "m2h", ALU.add)
-            mul("u2", "s4", "q2")
-            lin("w2", "u2", 1.0, t4)
-            mul("v2", "w2", "k1s")
-            i2 = inv("j", "v2", -1.0, 1.0, 1.0)
+            k1 = inv("i", "u1", -2.0 / m0, 1.0 - 2.0 / m0 * t2, 2.0 / m0,
+                     [lambda: fma("u2", mean, ALU.mult, n, ALU.mult, "q2")])
+            mul("q4", "q2", "q2")
+            mul("k1s", k1, k1)
+            mul("u3", "s8", "q4")
+            fma("v2", "u2", ALU.add, t4, ALU.mult, "k1s")
+            i2 = inv("j", "v2", -1.0, 1.0, 1.0, [lambda: lin("nr", "r", -1.0, 0.0)])
             mul("k2", "k1s", i2)
             mul("k2s", "k2", "k2")
-            mul("q4", "q2", "q2")
-            mul("u3", "s8", "q4")
-            lin("w3", "u3", 1.0, t8)
-            mul("v3", "w3", "k2s")
-            i3 = inv("k", "v3", -1.0, 1.0, 1.0)
-            lin("k2t", "k2s", t8, 0.0)
-            mul(cond[g], "k2t", i3)
-            lin("d", cond[g], -1.0, 1.0)
-            mul(alpha[g], "d", "r")
+            fma("v3", "u3", ALU.add, t8, ALU.mult, "k2s")
+            i3 = inv("k", "v3", -1.0, 1.0, 1.0, [lambda: lin("k2t", "k2s", t8, 0.0)])
+            mul("cond", "k2t", i3)
+            fma("alpha", "cond", ALU.subtract, 1.0, ALU.mult, "nr")
             return ops
 
-        def first_term(i):
-            t1[i] = work.tile([P, BLK, C], F32, name="t1", bufs=5)
-            for b in range(BLK):
-                g, c = col(i, b)
-                nc.gpsimd.tensor_scalar(out=t1[i][:, b, :], in0=ez[0, i][:, b, :], scalar1=alpha[g][:, c : c + 1], scalar2=0.0, op0=ALU.mult, op1=ALU.add)
-
-        def recip2(i):
-            rz2[i] = work.tile([P, BLK], F32, name="rz2", bufs=4)
-            nc.vector.reciprocal(out=rz2[i][:], in_=zsum2[i][:])
-            beta[i] = work.tile([P, BLK], F32, name="beta", bufs=4)
-            g, c = col(i, 0)
-            nc.gpsimd.tensor_tensor(out=beta[i][:], in0=rz2[i][:], in1=cond[g][:, c : c + BLK], op=ALU.mult)
-
-        def blend(i):
-            ob = work.tile([P, BLK, C], F32, name="ob", bufs=4)
-            for b in range(BLK):
-                nc.vector.scalar_tensor_tensor(out=ob[:, b, :], in0=ez[1, i][:, b, :], scalar=beta[i][:, b : b + 1], in1=t1[i][:, b, :],
-                                               op0=ALU.mult, op1=ALU.add)
-            nc.sync.dma_start(out=out_rows[i], in_=ob[:])
+        def blend(units):
+            c0, c1 = BLK * units[0], BLK * (units[-1] + 1)
+            rz = work.tile([P, c1 - c0], F32, name="rz", bufs=2)
+            beta = work.tile([P, c1 - c0], F32, name="beta", bufs=2)
+            nc.vector.reciprocal(out=rz[:], in_=zsum2[:, c0:c1])
+            terms = {}
+            for i in units:
+                terms[i] = work.tile([P, BLK, C], F32, name="t1", bufs=3)
+                for b in range(BLK):
+                    c = BLK * i + b
+                    nc.vector.tensor_scalar(out=terms[i][:, b, :], in0=ez[0, i][:, b, :], scalar1=alpha[:, c : c + 1], scalar2=None, op0=ALU.mult)
+                if i == units[0]:
+                    nc.vector.tensor_tensor(out=beta[:], in0=rz[:], in1=cond[:, c0:c1], op=ALU.mult)
+            for i in units:
+                ob = work.tile([P, BLK, C], F32, name="ob", bufs=4)
+                for b in range(BLK):
+                    c = BLK * i + b - c0
+                    nc.vector.scalar_tensor_tensor(out=ob[:, b, :], in0=ez[1, i][:, b, :], scalar=beta[:, c : c + 1], in1=terms[i][:, b, :],
+                                                   op0=ALU.mult, op1=ALU.add)
+                nc.sync.dma_start(out=out_rows[i], in_=ob[:])
 
         w_raw, w_grp = {}, {}
 
@@ -312,14 +301,23 @@ def tile_combnethe_pa_t_kernel(tc, x_bytes, x_scale, W1o, b1o, W2o, b2o, W1f, b1
         items = [(0, i) for i in range(N_UNITS)] + [(1, i) for i in range(N_UNITS)]
         n_items = len(items)
         gate_ops = []
-        for q in range(n_items + 5):
+        blended = 0
+
+        def fill(k):
+            for op in gate_ops[:k]:
+                op()
+            del_count = min(k, len(gate_ops))
+            return gate_ops[del_count:]
+
+        for q in range(n_items + 4):
 
             def item(k):
                 return items[k] if 0 <= k < n_items else None
 
-            now, nxt, prev, prev2, prev3, prev4 = (item(q + d) for d in (0, 1, -1, -2, -3, -4))
-            if q + 6 < N_UNITS:
-                load(q + 6)
+            now, nxt, prev, prev2, prev3 = (item(q + d) for d in (0, 1, -1, -2, -3))
+            phase1 = now and now[0] == 0
+            if q + 5 < N_UNITS and q > 0:
+                load(q + 5)
             if now:
                 relu(*now)
             if nxt and nxt[0] == 1:
@@ -330,45 +328,48 @@ def tile_combnethe_pa_t_kernel(tc, x_bytes, x_scale, W1o, b1o, W2o, b2o, W1f, b1
                     turn(q + 2, h)
             if prev3 and prev3[0] == 0:
                 power_stats(prev3[1])
-                if prev3[1] % GATE_UNITS == GATE_UNITS - 1:
-                    gate_ops += gate(prev3[1] // GATE_UNITS)
-            if prev3 and prev3[0] == 1:
-                recip2(prev3[1])
+                if prev3[1] == N_UNITS - 1:
+                    gate_ops = gate()
             if prev2:
                 exps(*prev2)
-                if prev2[0] == 1:
-                    first_term(prev2[1])
             if prev:
                 logits(*prev)
                 turn_logits(*prev)
             if nxt and nxt[0] == 0:
                 quant_x(nxt[1])
                 mm1(*nxt)
+            gate_ops = fill(2)
             if now:
                 weave(*now)
             if q == 0:
                 nc.vector.quantize_mx(out=w2_codes[:].bitcast(FP8X4), scales=w2_scales[:], in_=w2_grp[:].rearrange("p n c j -> p (n c j)"))
-            if prev4 and prev4[0] == 1:
-                blend(prev4[1])
-            if now:
-                if now[0] == 0 and prev:
+            gate_ops = fill(2)
+            if phase1:
+                if prev:
                     rowmin(*prev)
+            elif q > N_UNITS + 2 and not gate_ops:
+                ready = min(q - N_UNITS - 2, N_UNITS)
+                units = list(range(blended, min(ready, blended + 2)))
+                if units and (len(units) == 2 or q >= n_items + 2 or True):
+                    blend(units)
+                    blended = units[-1] + 1
+            if now:
                 quant_h(*now)
                 mm2(*now)
-            if prev and not (now and now[0] == 0):
+            gate_ops = fill(2)
+            if prev and not phase1:
                 rowmin(*prev)
+            gate_ops = fill(2)
             if q == 6:
                 group_w1(1, nc.vector.tensor_copy)
             if q == 7:
                 quant_w1(1)
             if prev2 and prev2[0] == 0:
                 powers(prev2[1])
-            for op in gate_ops[:8]:
-                op()
-            gate_ops = gate_ops[8:]
             if q + 2 < N_UNITS:
                 leave(q + 2, 0)
             if prev2 and prev2[0] == 0:
                 fourth(prev2[1])
             if q + 2 < N_UNITS:
                 leave(q + 2, 1)
+        assert blended == N_UNITS

@@ -5,7 +5,6 @@ from concourse.masks import make_identity
 
 B, D_IN, D_H, C = 8192, 512, 512, 128
 FLOPS = 2 * (2 * B * D_IN * D_H + 2 * B * D_H * C)
-
 TAU = 0.5
 
 F32 = mybir.dt.float32
@@ -19,10 +18,20 @@ ALU = mybir.AluOpType
 AX = mybir.AxisListType
 
 P = 128
+PACK = 4
 UNIT = 512
 BLK = UNIT // P
 N_UNITS = B // UNIT
-GATE_UNITS = 16
+COLS = N_UNITS * BLK
+
+VA = 14
+VB = 21
+LM = 5
+LO = 0
+T1S = 13
+FILL = 1
+SPLIT = (4,)
+FIRST = (2, 2)
 
 
 def tile_combnethe_pa_t_kernel(tc, x_bytes, x_scale, W1o, b1o, W2o, b2o, W1f, b1f, W2f, b2f, out):
@@ -34,8 +43,7 @@ def tile_combnethe_pa_t_kernel(tc, x_bytes, x_scale, W1o, b1o, W2o, b2o, W1f, b1
     with ExitStack() as ctx:
         keep = ctx.enter_context(tc.tile_pool(name="keep", bufs=1))
         work = ctx.enter_context(tc.tile_pool(name="work", bufs=3))
-        psum = ctx.enter_context(tc.psum_pool(name="psum", bufs=2))
-        ctx.enter_context(tc.manual_schedule())
+        psum = ctx.enter_context(tc.psum_pool(name="psum", bufs=4))
 
         ident = keep.tile([P, P], F32, name="ident")
         scale = keep.tile([P, 2, D_IN], F32, name="scale")
@@ -43,46 +51,56 @@ def tile_combnethe_pa_t_kernel(tc, x_bytes, x_scale, W1o, b1o, W2o, b2o, W1f, b1
         w1_scales = [keep.tile([P, D_H], U8, name="w1s%d" % n, align_bytes=64) for n in range(2)]
         w2_codes = keep.tile([P, 2 * C], U32, name="w2c", align_bytes=64)
         w2_scales = keep.tile([P, 2 * C], U8, name="w2s", align_bytes=64)
-        b1 = [keep.tile([P, 4], BF16, name="b1_%d" % n) for n in range(2)]
+        b1 = [keep.tile([P, PACK], BF16, name="b1_%d" % n) for n in range(2)]
+        b1w = [keep.tile([P, PACK], F32, name="b1w_%d" % n) for n in range(2)]
         b2 = [keep.tile([P, 1], BF16, name="b2_%d" % n) for n in range(2)]
         b2n = [keep.tile([P, 1], F32, name="b2n_%d" % n) for n in range(2)]
         warm = keep.tile([P, 1], F32, name="warm")
+        w_raw = [keep.tile([P, PACK, D_H], BF16, name="w1raw%d" % n) for n in range(2)]
+        w_grp = [keep.tile([P, D_H, PACK], BF16, name="w1grp%d" % n, align_bytes=64) for n in range(2)]
+        w2_raw = keep.tile([P, 2, PACK, C], BF16, name="w2raw")
+        w2_grp = keep.tile([P, 2, C, PACK], BF16, name="w2grp", align_bytes=64)
+        zsum = [keep.tile([P, COLS], F32, name="zsum%d" % n) for n in range(2)]
+        sum2 = keep.tile([P, COLS], F32, name="sum2")
+        stats = keep.tile([P, COLS // 2, 2, 3], F32, name="stats")
+        alpha = keep.tile([P, COLS], F32, name="alpha")
+        cond = keep.tile([P, COLS], F32, name="cond")
 
         xb, xs, xt, xg, xq = {}, {}, {}, {}, {}
-        ps1, hp, hg, hq, ps2, zt, zl, nm, ez, e2s, e4 = {}, {}, {}, {}, {}, {}, {}, {}, {}, {}, {}
-
-        cols = N_UNITS * BLK
-        zsum = keep.tile([P, cols], F32, name="zsum")
-        s2 = keep.tile([P, cols], F32, name="s2")
-        stats = keep.tile([P, cols // 2, 2, 3], F32, name="stats")
-        alpha = keep.tile([P, cols], F32, name="alpha")
-        cond = keep.tile([P, cols], F32, name="cond")
-        zsum2 = keep.tile([P, cols], F32, name="zsum2")
+        ps1, hp, hg, hq, ps2, zl, zt, nm, ez, e2, e4, t1 = {}, {}, {}, {}, {}, {}, {}, {}, {}, {}, {}, {}
 
         def load(i):
-            t = work.tile([P, BLK, D_IN], U8, name="xb", bufs=6)
-            nc.sync.dma_start(out=t[:], in_=x_rows[i])
-            xb[i] = t
+            xb[i] = work.tile([P, BLK, D_IN], U8, name="xb", bufs=6)
+            nc.sync.dma_start(out=xb[i][:], in_=x_rows[i])
+
+        def load_w1(n):
+            nc.sync.dma_start(out=w_raw[n][:], in_=w1_in[n].rearrange("(p j) c -> p j c", j=PACK))
+
+        def group_w1(n):
+            nc.scalar.copy(out=w_grp[n][:].rearrange("p (t m) j -> p t m j", t=PACK), in_=w_raw[n][:].rearrange("p j (m t) -> p t m j", t=PACK))
+
+        def quant_w1(n):
+            nc.vector.quantize_mx(out=w1_codes[n][:].bitcast(FP8X4), scales=w1_scales[n][:], in_=w_grp[n][:].rearrange("p c j -> p (c j)"))
 
         def widen(i, h):
-            t = work.tile([P, 2, D_IN], BF16, name="xs", bufs=4, align_bytes=64)
+            xs[i, h] = work.tile([P, 2, D_IN], BF16, name="xs", bufs=4, align_bytes=64)
             nc.vector.tensor_tensor(
-                out=t[:].rearrange("p b k -> p (b k)"),
+                out=xs[i, h][:].rearrange("p b k -> p (b k)"),
                 in0=xb[i][:, 2 * h : 2 * h + 2, :].rearrange("p b k -> p (b k)").bitcast(FP8),
-                in1=scale[:].rearrange("p b k -> p (b k)"), op=ALU.mult)
-            xs[i, h] = t
+                in1=scale[:].rearrange("p b k -> p (b k)"),
+                op=ALU.mult,
+            )
 
         def turn(i, h):
-            t = psum.tile([P, 2, 2, P], F32, name="xt", bufs=2)
+            xt[i, h] = psum.tile([P, 2, 2, P], F32, name="xt", tag="aux", bufs=4)
             words = xs[i, h][:].rearrange("p b k -> p (b k)").bitcast(F32)
             for b in range(2):
                 for u in range(2):
-                    nc.tensor.transpose(t[:, b, u, :], words[:, 256 * b + u : 256 * (b + 1) : 2], ident[:])
-            xt[i, h] = t
+                    nc.tensor.transpose(xt[i, h][:, b, u, :], words[:, 256 * b + u : 256 * (b + 1) : 2], ident[:])
 
         def leave(i, h):
             if h == 0:
-                xg[i] = work.tile([P, UNIT, 4], BF16, name="xg", bufs=3, align_bytes=64)
+                xg[i] = work.tile([P, UNIT, PACK], BF16, name="xg", bufs=3, align_bytes=64)
             words = xg[i][:].rearrange("p n j -> p (n j)").bitcast(F32).rearrange("p (b r u) -> p b r u", b=BLK, u=2)
             nc.scalar.copy(out=words[:, 2 * h : 2 * h + 2], in_=xt[i, h][:].rearrange("p b u r -> p b r u"))
 
@@ -92,84 +110,93 @@ def tile_combnethe_pa_t_kernel(tc, x_bytes, x_scale, W1o, b1o, W2o, b2o, W1f, b1
             nc.vector.quantize_mx(out=codes[:].bitcast(FP8X4), scales=scales[:], in_=xg[i][:].rearrange("p n j -> p (n j)"))
             xq[i] = (codes, scales)
 
-        def mm1(n, i):
+        def mm1(it):
+            n, i, b0, nb = it
             codes, scales = xq[i]
-            for t in range(4):
-                acc = psum.tile([P, UNIT], F32, name="ps1", bufs=4)
+            tok = slice(P * b0, P * (b0 + nb))
+            for t in range(PACK):
+                acc = psum.tile([P, P * nb], F32, name="ps1", bufs=4)
                 m = slice(P * t, P * (t + 1))
                 nc.tensor.matmul_mx(out=acc[:], lhsT=w1_codes[n][:, m].bitcast(FP8X4), lhsT_scale=w1_scales[n][:, m],
-                                    rhs=codes[:].bitcast(FP8X4), rhs_scale=scales[:], start=True, stop=True)
-                ps1[n, i, t] = acc
+                                    rhs=codes[:, tok].bitcast(FP8X4), rhs_scale=scales[:, tok], start=True, stop=True)
+                ps1[it, t] = acc
 
-        def relu(n, i):
-            hp[n, i] = work.tile([P, 4, UNIT], BF16, name="hp", bufs=3, align_bytes=64)
-            for t in range(4):
-                nc.scalar.activation(hp[n, i][:, t, :], ps1[n, i, t][:], ACT.Relu, bias=b1[n][:, t : t + 1])
+        def relu(it, on_vector):
+            n, i, b0, nb = it
+            hp[it] = work.tile([P, PACK, P * nb], BF16, name="hp", bufs=3, align_bytes=64)
+            for t in range(PACK):
+                if t < PACK - on_vector:
+                    nc.scalar.activation(hp[it][:, t, :], ps1[it, t][:], ACT.Relu, bias=b1[n][:, t : t + 1])
+                else:
+                    nc.vector.tensor_scalar(out=hp[it][:, t, :], in0=ps1[it, t][:], scalar1=b1w[n][:, t : t + 1], scalar2=0.0, op0=ALU.add, op1=ALU.max)
 
-        def weave(n, i):
-            hg[n, i] = work.tile([P, UNIT, 4], BF16, name="hg", bufs=3, align_bytes=64)
-            nc.vector.tensor_copy(out=hg[n, i][:].rearrange("p (c i) t -> p c t i", i=4),
-                                  in_=hp[n, i][:].rearrange("p t (c i) -> p c t i", i=4))
+        def weave(it):
+            hg[it] = work.tile([P, P * it[3], PACK], BF16, name="hg", bufs=3, align_bytes=64)
+            nc.vector.tensor_copy(out=hg[it][:].rearrange("p (c i) t -> p c t i", i=4), in_=hp[it][:].rearrange("p t (c i) -> p c t i", i=4))
 
-        def quant_h(n, i):
-            codes = work.tile([P, UNIT], U32, name="hq", bufs=3, align_bytes=64)
-            scales = work.tile([P, UNIT], U8, name="hqs", bufs=3, align_bytes=64)
-            nc.vector.quantize_mx(out=codes[:].bitcast(FP8X4), scales=scales[:], in_=hg[n, i][:].rearrange("p n j -> p (n j)"))
-            hq[n, i] = (codes, scales)
+        def quant_h(it):
+            codes = work.tile([P, P * it[3]], U32, name="hq", bufs=3, align_bytes=64)
+            scales = work.tile([P, P * it[3]], U8, name="hqs", bufs=3, align_bytes=64)
+            nc.vector.quantize_mx(out=codes[:].bitcast(FP8X4), scales=scales[:], in_=hg[it][:].rearrange("p n j -> p (n j)"))
+            hq[it] = (codes, scales)
 
-        def mm2(n, i):
-            codes, scales = hq[n, i]
-            acc = psum.tile([P, UNIT], F32, name="ps2", bufs=1)
+        def mm2(it):
+            n, i, b0, nb = it
+            codes, scales = hq[it]
+            ps2[it] = psum.tile([P, P * nb], F32, name="ps2", tag="aux", bufs=4)
             w = slice(C * n, C * (n + 1))
-            nc.tensor.matmul_mx(out=acc[:], lhsT=w2_codes[:, w].bitcast(FP8X4), lhsT_scale=w2_scales[:, w],
+            nc.tensor.matmul_mx(out=ps2[it][:], lhsT=w2_codes[:, w].bitcast(FP8X4), lhsT_scale=w2_scales[:, w],
                                 rhs=codes[:].bitcast(FP8X4), rhs_scale=scales[:], start=True, stop=True)
-            ps2[n, i] = acc
 
-        def logits(n, i):
-            zl[n, i] = work.tile([P, UNIT], F32, name="zl", bufs=2)
-            nc.scalar.activation(zl[n, i][:], ps2[n, i][:], ACT.Identity, bias=b2n[n][:], scale=-1.0)
+        def logits(it, on_vector):
+            n, i, b0, nb = it
+            zl[it] = work.tile([P, P * nb], F32, name="zl", bufs=2)
+            if on_vector:
+                nc.vector.tensor_scalar(out=zl[it][:], in0=ps2[it][:], scalar1=-1.0, scalar2=b2n[n][:], op0=ALU.mult, op1=ALU.add)
+            else:
+                nc.scalar.activation(zl[it][:], ps2[it][:], ACT.Identity, bias=b2n[n][:], scale=-1.0)
 
-        def turn_logits(n, i):
-            zt[n, i] = psum.tile([P, BLK, C], F32, name="zt", bufs=1)
-            for b in range(BLK):
-                nc.tensor.transpose(zt[n, i][:, b, :], zl[n, i][:, P * b : P * (b + 1)], ident[:])
+        def turn_logits(it):
+            zt[it] = psum.tile([P, it[3], C], F32, name="zt", tag="aux", bufs=4)
+            for b in range(it[3]):
+                nc.tensor.transpose(zt[it][:, b, :], zl[it][:, P * b : P * (b + 1)], ident[:])
 
-        def rowmin(n, i):
-            nm[n, i] = work.tile([P, BLK], F32, name="nm", bufs=4)
-            nc.vector.tensor_reduce(out=nm[n, i][:], in_=zt[n, i][:], axis=AX.X, op=ALU.min)
+        def rowmin(it):
+            nm[it] = work.tile([P, it[3]], F32, name="nm", bufs=4)
+            nc.vector.tensor_reduce(out=nm[it][:], in_=zt[it][:], axis=AX.X, op=ALU.min)
 
-        def exps(n, i):
-            ez[n, i] = work.tile([P, BLK, C], F32, name="ez%d" % n, bufs=N_UNITS if n == 0 else 9)
-            acc = zsum if n == 0 else zsum2
-            for b in range(BLK):
-                c = BLK * i + b
-                nc.scalar.activation(ez[n, i][:, b, :], zt[n, i][:, b, :], ACT.Exp, bias=nm[n, i][:, b : b + 1], scale=-1.0, accum_out=acc[:, c : c + 1])
+        def exps(it):
+            n, i, b0, nb = it
+            ez[it] = work.tile([P, nb, C], F32, name="ez%d" % n, bufs=N_UNITS if n == 0 else 9)
+            for b in range(nb):
+                c = BLK * i + b0 + b
+                nc.scalar.activation(ez[it][:, b, :], zt[it][:, b, :], ACT.Exp, bias=nm[it][:, b : b + 1], scale=-1.0, accum_out=zsum[n][:, c : c + 1])
 
-        def powers(i):
-            e2 = work.tile([P, BLK, C], F32, name="e2", bufs=2)
-            for b in range(BLK):
-                c = BLK * i + b
-                nc.scalar.activation(e2[:, b, :], ez[0, i][:, b, :], ACT.Square, accum_out=s2[:, c : c + 1])
-            e2s[i] = e2
+        def squares(it):
+            n, i, b0, nb = it
+            e2[it] = work.tile([P, nb, C], F32, name="e2", bufs=2)
+            for b in range(nb):
+                c = BLK * i + b0 + b
+                nc.scalar.activation(e2[it][:, b, :], ez[it][:, b, :], ACT.Square, accum_out=sum2[:, c : c + 1])
 
-        def fourth(i):
-            e4[i] = work.tile([P, BLK, C], F32, name="e4", bufs=3)
-            nc.scalar.activation(e4[i][:], e2s[i][:], ACT.Square)
+        def fourth_powers(it):
+            e4[it] = work.tile([P, it[3], C], F32, name="e4", bufs=3)
+            nc.scalar.activation(e4[it][:], e2[it][:], ACT.Square)
 
-        def power_stats(i):
-            for h in range(2):
-                nc.vector.bn_stats(out=stats[:, 2 * i + h].rearrange("p b s -> p (b s)"), in_=e4[i][:, 2 * h : 2 * h + 2, :].rearrange("p b c -> p c b"))
+        def power_stats(it):
+            n, i, b0, nb = it
+            for h in range(0, nb, 2):
+                nc.vector.bn_stats(out=stats[:, (BLK * i + b0 + h) // 2].rearrange("p b s -> p (b s)"), in_=e4[it][:, h : h + 2, :].rearrange("p b c -> p c b"))
 
         def gate():
-            t = {}
+            t = {"z": zsum[0], "s2": sum2, "cond": cond, "alpha": alpha}
             ops = []
             per = stats[:].rearrange("p g b s -> p (g b) s")
             mean, m2 = per[:, :, 1], per[:, :, 2]
-            t["z"], t["s2"], t["cond"], t["alpha"] = zsum, s2, cond, alpha
 
             def new(key):
                 if key not in t:
-                    t[key] = work.tile([P, cols], F32, name="g_" + key, bufs=1)
+                    t[key] = work.tile([P, COLS], F32, name="g_" + key, bufs=1)
                 return t[key][:]
 
             def val(a):
@@ -191,8 +218,7 @@ def tile_combnethe_pa_t_kernel(tc, x_bytes, x_scale, W1o, b1o, W2o, b2o, W1f, b1
                 lin("y" + r, v, vm, vc)
                 lin("a" + r, v, vm * two_over_m, (vc + 1.0) * two_over_m)
                 mul("y2" + r, "y" + r, "y" + r)
-                for f in extra:
-                    f()
+                extra()
                 mul("y4" + r, "y2" + r, "y2" + r)
                 fma("b" + r, "y2" + r, ALU.add, 1.0, ALU.mult, "a" + r)
                 mul("y8" + r, "y4" + r, "y4" + r)
@@ -209,54 +235,47 @@ def tile_combnethe_pa_t_kernel(tc, x_bytes, x_scale, W1o, b1o, W2o, b2o, W1f, b1
             fma("s8", "msq", ALU.mult, n, ALU.add, m2)
             mul("u1", "s2", "q")
             mul("q2", "q", "q")
-            k1 = inv("i", "u1", -2.0 / m0, 1.0 - 2.0 / m0 * t2, 2.0 / m0,
-                     [lambda: fma("u2", mean, ALU.mult, n, ALU.mult, "q2")])
+            k1 = inv("i", "u1", -2.0 / m0, 1.0 - 2.0 / m0 * t2, 2.0 / m0, lambda: fma("u2", mean, ALU.mult, n, ALU.mult, "q2"))
             mul("q4", "q2", "q2")
             mul("k1s", k1, k1)
             mul("u3", "s8", "q4")
             fma("v2", "u2", ALU.add, t4, ALU.mult, "k1s")
-            i2 = inv("j", "v2", -1.0, 1.0, 1.0, [lambda: lin("nr", "r", -1.0, 0.0)])
+            i2 = inv("j", "v2", -1.0, 1.0, 1.0, lambda: lin("nr", "r", -1.0, 0.0))
             mul("k2", "k1s", i2)
             mul("k2s", "k2", "k2")
             fma("v3", "u3", ALU.add, t8, ALU.mult, "k2s")
-            i3 = inv("k", "v3", -1.0, 1.0, 1.0, [lambda: lin("k2t", "k2s", t8, 0.0)])
+            i3 = inv("k", "v3", -1.0, 1.0, 1.0, lambda: lin("k2t", "k2s", t8, 0.0))
             mul("cond", "k2t", i3)
             fma("alpha", "cond", ALU.subtract, 1.0, ALU.mult, "nr")
             return ops
 
-        def blend(units):
-            c0, c1 = BLK * units[0], BLK * (units[-1] + 1)
+        def first_term(it, on_vector):
+            n, i, b0, nb = it
+            t1[it] = work.tile([P, nb, C], F32, name="t1", bufs=5)
+            for b in range(nb):
+                a = alpha[:, BLK * i + b0 + b : BLK * i + b0 + b + 1]
+                if on_vector:
+                    nc.vector.tensor_scalar(out=t1[it][:, b, :], in0=ez[0, i, 0, BLK][:, b0 + b, :], scalar1=a, scalar2=None, op0=ALU.mult)
+                else:
+                    nc.scalar.activation(t1[it][:, b, :], ez[0, i, 0, BLK][:, b0 + b, :], ACT.Copy, scale=a)
+
+        def blend(group):
+            c0 = BLK * group[0][1] + group[0][2]
+            c1 = BLK * group[-1][1] + group[-1][2] + group[-1][3]
             rz = work.tile([P, c1 - c0], F32, name="rz", bufs=2)
             beta = work.tile([P, c1 - c0], F32, name="beta", bufs=2)
-            nc.vector.reciprocal(out=rz[:], in_=zsum2[:, c0:c1])
-            terms = {}
-            for i in units:
-                terms[i] = work.tile([P, BLK, C], F32, name="t1", bufs=3)
-                for b in range(BLK):
-                    c = BLK * i + b
-                    nc.vector.tensor_scalar(out=terms[i][:, b, :], in0=ez[0, i][:, b, :], scalar1=alpha[:, c : c + 1], scalar2=None, op0=ALU.mult)
-                if i == units[0]:
-                    nc.vector.tensor_tensor(out=beta[:], in0=rz[:], in1=cond[:, c0:c1], op=ALU.mult)
-            for i in units:
-                ob = work.tile([P, BLK, C], F32, name="ob", bufs=4)
-                for b in range(BLK):
-                    c = BLK * i + b - c0
-                    nc.vector.scalar_tensor_tensor(out=ob[:, b, :], in0=ez[1, i][:, b, :], scalar=beta[:, c : c + 1], in1=terms[i][:, b, :],
-                                                   op0=ALU.mult, op1=ALU.add)
-                nc.sync.dma_start(out=out_rows[i], in_=ob[:])
-
-        w_raw, w_grp = {}, {}
-
-        def load_w1(n):
-            w_raw[n] = keep.tile([P, 4, D_H], BF16, name="w1raw%d" % n)
-            nc.sync.dma_start(out=w_raw[n][:], in_=w1_in[n].rearrange("(p j) c -> p j c", j=4))
-
-        def group_w1(n, copy):
-            w_grp[n] = keep.tile([P, D_H, 4], BF16, name="w1grp%d" % n, align_bytes=64)
-            copy(out=w_grp[n][:].rearrange("p (t m) j -> p t m j", t=4), in_=w_raw[n][:].rearrange("p j (m t) -> p t m j", t=4))
-
-        def quant_w1(n):
-            nc.vector.quantize_mx(out=w1_codes[n][:].bitcast(FP8X4), scales=w1_scales[n][:], in_=w_grp[n][:].rearrange("p c j -> p (c j)"))
+            nc.vector.reciprocal(out=rz[:], in_=zsum[1][:, c0:c1])
+            todo = [it for it in group if it not in t1]
+            for it in todo:
+                first_term(it, True)
+            nc.vector.tensor_tensor(out=beta[:], in0=rz[:], in1=cond[:, c0:c1], op=ALU.mult)
+            for it in group:
+                n, i, b0, nb = it
+                ob = work.tile([P, nb, C], F32, name="ob", bufs=4)
+                for b in range(nb):
+                    c = BLK * i + b0 + b - c0
+                    nc.vector.scalar_tensor_tensor(out=ob[:, b, :], in0=ez[it][:, b, :], scalar=beta[:, c : c + 1], in1=t1[it][:, b, :], op0=ALU.mult, op1=ALU.add)
+                nc.sync.dma_start(out=out_rows[i][:, b0 : b0 + nb, :], in_=ob[:])
 
         nc.vector.memset(warm[:], 0.0)
         make_identity(nc, ident[:])
@@ -264,20 +283,17 @@ def tile_combnethe_pa_t_kernel(tc, x_bytes, x_scale, W1o, b1o, W2o, b2o, W1f, b1
         load(0)
         load_w1(0)
         load(1)
-        w2_raw = keep.tile([P, 2, 4, C], BF16, name="w2raw")
         for n in range(2):
-            nc.sync.dma_start(out=w2_raw[:, n], in_=w2_in[n].rearrange("(p j) c -> p j c", j=4))
+            nc.sync.dma_start(out=w2_raw[:, n], in_=w2_in[n].rearrange("(p j) c -> p j c", j=PACK))
         load(2)
-        load(3)
-        for n in range(2):
-            nc.scalar.dma_start(out=b1[n][:], in_=b1_in[n].rearrange("(p t) -> p t", t=4))
-        for n in range(2):
-            nc.scalar.dma_start(out=b2[n][:], in_=b2_in[n].rearrange("(c o) -> c o", o=1))
         load_w1(1)
-        load(4)
-        load(5)
+        for n in range(2):
+            nc.scalar.dma_start(out=b1[n][:], in_=b1_in[n].rearrange("(p t) -> p t", t=PACK))
+            nc.scalar.dma_start(out=b2[n][:], in_=b2_in[n].rearrange("(c o) -> c o", o=1))
+        for i in range(3, 6):
+            load(i)
         nc.scalar.activation(warm[:], warm[:], ACT.Exp)
-        group_w1(0, nc.scalar.copy)
+        group_w1(0)
         nc.vector.tensor_copy(out=scale[:, 1, :], in_=scale[:, 0, :])
         for h in range(2):
             widen(0, h)
@@ -286,90 +302,112 @@ def tile_combnethe_pa_t_kernel(tc, x_bytes, x_scale, W1o, b1o, W2o, b2o, W1f, b1
         widen(1, 0)
         turn(1, 0)
         quant_w1(0)
+        quant_x(0)
+
+        items = [(0, i, 0, BLK) for i in range(N_UNITS)] + [(1, i, 0, BLK) for i in range(N_UNITS - 1)]
+        b0 = 0
+        for nb in SPLIT:
+            items.append((1, N_UNITS - 1, b0, nb))
+            b0 += nb
+        mm1(items[0])
         widen(1, 1)
         turn(1, 1)
-        quant_x(0)
-        mm1(0, 0)
         for n in range(2):
+            nc.vector.tensor_copy(out=b1w[n][:], in_=b1[n][:])
             nc.vector.tensor_scalar(out=b2n[n][:], in0=b2[n][:], scalar1=-1.0, scalar2=None, op0=ALU.mult)
-        for h in range(2):
-            leave(1, h)
-        w2_grp = keep.tile([P, 2, C, 4], BF16, name="w2grp", align_bytes=64)
+        leave(1, 0)
         for n in range(2):
-            nc.vector.tensor_copy(out=w2_grp[:, n], in_=w2_raw[:, n].rearrange("p j c -> p c j"))
+            nc.scalar.copy(out=w2_grp[:, n], in_=w2_raw[:, n].rearrange("p j c -> p c j"))
 
-        items = [(0, i) for i in range(N_UNITS)] + [(1, i) for i in range(N_UNITS)]
         n_items = len(items)
         gate_ops = []
-        blended = 0
+        done = N_UNITS
 
-        def fill(k):
-            for op in gate_ops[:k]:
+        def run_gate():
+            for op in gate_ops[:FILL]:
                 op()
-            del_count = min(k, len(gate_ops))
-            return gate_ops[del_count:]
+            return gate_ops[FILL:]
 
         for q in range(n_items + 4):
 
-            def item(k):
-                return items[k] if 0 <= k < n_items else None
+            def o(k):
+                return items[k] if 0 <= k < N_UNITS else None
 
-            now, nxt, prev, prev2, prev3 = (item(q + d) for d in (0, 1, -1, -2, -3))
-            phase1 = now and now[0] == 0
-            if q + 5 < N_UNITS and q > 0:
+            def f(k):
+                return items[k] if N_UNITS <= k < n_items else None
+
+            now, nxt = o(q) or f(q), o(q + 1) or f(q + 1)
+            if 1 <= q < N_UNITS - 5:
                 load(q + 5)
             if now:
-                relu(*now)
-            if nxt and nxt[0] == 1:
-                mm1(*nxt)
+                relu(now, 1 if VA <= q < VB else 0)
+            if q == 0:
+                leave(1, 1)
+            if f(q + 1):
+                mm1(nxt)
             if q + 2 < N_UNITS:
                 for h in range(2):
                     widen(q + 2, h)
                     turn(q + 2, h)
-            if prev3 and prev3[0] == 0:
-                power_stats(prev3[1])
-                if prev3[1] == N_UNITS - 1:
+            if o(q - 3):
+                power_stats(o(q - 3))
+                if q - 3 == N_UNITS - 1:
                     gate_ops = gate()
-            if prev2:
-                exps(*prev2)
-            if prev:
-                logits(*prev)
-                turn_logits(*prev)
-            if nxt and nxt[0] == 0:
-                quant_x(nxt[1])
-                mm1(*nxt)
-            gate_ops = fill(2)
-            if now:
-                weave(*now)
+            if f(q - 3):
+                rowmin(f(q - 3))
+            if o(q - 2):
+                exps(o(q - 2))
+            if f(q - 2):
+                logits(f(q - 2), (q - 2) % LM == LO)
+                turn_logits(f(q - 2))
+            if f(q - 3):
+                exps(f(q - 3))
+                if f(q - 3)[1] >= T1S:
+                    first_term(f(q - 3), False)
+            if o(q - 1):
+                logits(o(q - 1), (q - 1) % LM == LO)
+                turn_logits(o(q - 1))
+            if o(q + 1):
+                quant_x(q + 1)
+                mm1(nxt)
+            gate_ops = run_gate()
+            if o(q):
+                weave(o(q))
+            if f(q - 1):
+                weave(f(q - 1))
             if q == 0:
                 nc.vector.quantize_mx(out=w2_codes[:].bitcast(FP8X4), scales=w2_scales[:], in_=w2_grp[:].rearrange("p n c j -> p (n c j)"))
-            gate_ops = fill(2)
-            if phase1:
-                if prev:
-                    rowmin(*prev)
-            elif q > N_UNITS + 2 and not gate_ops:
-                ready = min(q - N_UNITS - 2, N_UNITS)
-                units = list(range(blended, min(ready, blended + 2)))
-                if units and (len(units) == 2 or q >= n_items + 2 or True):
-                    blend(units)
-                    blended = units[-1] + 1
-            if now:
-                quant_h(*now)
-                mm2(*now)
-            gate_ops = fill(2)
-            if prev and not phase1:
-                rowmin(*prev)
-            gate_ops = fill(2)
-            if q == 6:
-                group_w1(1, nc.vector.tensor_copy)
-            if q == 7:
+                group_w1(1)
+            if q == 13:
                 quant_w1(1)
-            if prev2 and prev2[0] == 0:
-                powers(prev2[1])
+            gate_ops = run_gate()
+            if o(q - 1):
+                rowmin(o(q - 1))
+
+            def blend_some(done, upto):
+                group = items[done : max(done, min(upto, done + 2))]
+                if group:
+                    blend(group)
+                return done + len(group)
+
+            if q > N_UNITS + 3 and q < n_items and not gate_ops:
+                done = blend_some(done, q - 3)
+            if o(q):
+                quant_h(o(q))
+                mm2(o(q))
+            if f(q - 1):
+                quant_h(f(q - 1))
+                mm2(f(q - 1))
+            gate_ops = run_gate()
+            if q >= n_items:
+                done = blend_some(done, q - 2)
+            gate_ops = run_gate()
+            if o(q - 2):
+                squares(o(q - 2))
             if q + 2 < N_UNITS:
                 leave(q + 2, 0)
-            if prev2 and prev2[0] == 0:
-                fourth(prev2[1])
+            if o(q - 2):
+                fourth_powers(o(q - 2))
             if q + 2 < N_UNITS:
                 leave(q + 2, 1)
-        assert blended == N_UNITS
+        assert done == n_items

@@ -25,13 +25,23 @@ N_UNITS = B // UNIT
 COLS = N_UNITS * BLK
 
 VA = 14
-VB = 21
-LM = 5
-LO = 0
-T1S = 13
-FILL = 1
+VB = 23
+LM = 6
+LO = 2
+T1S = 8
+FILL = 2
 SPLIT = (4,)
-FIRST = (2, 2)
+GW = 0
+QW = 8
+PSA = 4
+HB = 3
+ZB = 3
+LW = 0
+LG = 1
+LX = 3
+SQ = 1
+EF = 1
+LA = 2
 
 
 def tile_combnethe_pa_t_kernel(tc, x_bytes, x_scale, W1o, b1o, W2o, b2o, W1f, b1f, W2f, b2f, out):
@@ -92,7 +102,7 @@ def tile_combnethe_pa_t_kernel(tc, x_bytes, x_scale, W1o, b1o, W2o, b2o, W1f, b1
             )
 
         def turn(i, h):
-            xt[i, h] = psum.tile([P, 2, 2, P], F32, name="xt", tag="aux", bufs=4)
+            xt[i, h] = psum.tile([P, 2, 2, P], F32, name="xt", tag="aux", bufs=PSA)
             words = xs[i, h][:].rearrange("p b k -> p (b k)").bitcast(F32)
             for b in range(2):
                 for u in range(2):
@@ -100,7 +110,7 @@ def tile_combnethe_pa_t_kernel(tc, x_bytes, x_scale, W1o, b1o, W2o, b2o, W1f, b1
 
         def leave(i, h):
             if h == 0:
-                xg[i] = work.tile([P, UNIT, PACK], BF16, name="xg", bufs=3, align_bytes=64)
+                xg[i] = work.tile([P, UNIT, PACK], BF16, name="xg", bufs=HB, align_bytes=64)
             words = xg[i][:].rearrange("p n j -> p (n j)").bitcast(F32).rearrange("p (b r u) -> p b r u", b=BLK, u=2)
             nc.scalar.copy(out=words[:, 2 * h : 2 * h + 2], in_=xt[i, h][:].rearrange("p b u r -> p b r u"))
 
@@ -115,7 +125,7 @@ def tile_combnethe_pa_t_kernel(tc, x_bytes, x_scale, W1o, b1o, W2o, b2o, W1f, b1
             codes, scales = xq[i]
             tok = slice(P * b0, P * (b0 + nb))
             for t in range(PACK):
-                acc = psum.tile([P, P * nb], F32, name="ps1", bufs=4)
+                acc = psum.tile([P, P * nb], F32, name="ps1", bufs=8 - PSA)
                 m = slice(P * t, P * (t + 1))
                 nc.tensor.matmul_mx(out=acc[:], lhsT=w1_codes[n][:, m].bitcast(FP8X4), lhsT_scale=w1_scales[n][:, m],
                                     rhs=codes[:, tok].bitcast(FP8X4), rhs_scale=scales[:, tok], start=True, stop=True)
@@ -123,7 +133,7 @@ def tile_combnethe_pa_t_kernel(tc, x_bytes, x_scale, W1o, b1o, W2o, b2o, W1f, b1
 
         def relu(it, on_vector):
             n, i, b0, nb = it
-            hp[it] = work.tile([P, PACK, P * nb], BF16, name="hp", bufs=3, align_bytes=64)
+            hp[it] = work.tile([P, PACK, P * nb], BF16, name="hp", bufs=HB, align_bytes=64)
             for t in range(PACK):
                 if t < PACK - on_vector:
                     nc.scalar.activation(hp[it][:, t, :], ps1[it, t][:], ACT.Relu, bias=b1[n][:, t : t + 1])
@@ -131,7 +141,7 @@ def tile_combnethe_pa_t_kernel(tc, x_bytes, x_scale, W1o, b1o, W2o, b2o, W1f, b1
                     nc.vector.tensor_scalar(out=hp[it][:, t, :], in0=ps1[it, t][:], scalar1=b1w[n][:, t : t + 1], scalar2=0.0, op0=ALU.add, op1=ALU.max)
 
         def weave(it):
-            hg[it] = work.tile([P, P * it[3], PACK], BF16, name="hg", bufs=3, align_bytes=64)
+            hg[it] = work.tile([P, P * it[3], PACK], BF16, name="hg", bufs=HB, align_bytes=64)
             nc.vector.tensor_copy(out=hg[it][:].rearrange("p (c i) t -> p c t i", i=4), in_=hp[it][:].rearrange("p t (c i) -> p c t i", i=4))
 
         def quant_h(it):
@@ -143,21 +153,21 @@ def tile_combnethe_pa_t_kernel(tc, x_bytes, x_scale, W1o, b1o, W2o, b2o, W1f, b1
         def mm2(it):
             n, i, b0, nb = it
             codes, scales = hq[it]
-            ps2[it] = psum.tile([P, P * nb], F32, name="ps2", tag="aux", bufs=4)
+            ps2[it] = psum.tile([P, P * nb], F32, name="ps2", tag="aux", bufs=PSA)
             w = slice(C * n, C * (n + 1))
             nc.tensor.matmul_mx(out=ps2[it][:], lhsT=w2_codes[:, w].bitcast(FP8X4), lhsT_scale=w2_scales[:, w],
                                 rhs=codes[:].bitcast(FP8X4), rhs_scale=scales[:], start=True, stop=True)
 
         def logits(it, on_vector):
             n, i, b0, nb = it
-            zl[it] = work.tile([P, P * nb], F32, name="zl", bufs=2)
+            zl[it] = work.tile([P, P * nb], F32, name="zl", bufs=ZB)
             if on_vector:
                 nc.vector.tensor_scalar(out=zl[it][:], in0=ps2[it][:], scalar1=-1.0, scalar2=b2n[n][:], op0=ALU.mult, op1=ALU.add)
             else:
                 nc.scalar.activation(zl[it][:], ps2[it][:], ACT.Identity, bias=b2n[n][:], scale=-1.0)
 
         def turn_logits(it):
-            zt[it] = psum.tile([P, it[3], C], F32, name="zt", tag="aux", bufs=4)
+            zt[it] = psum.tile([P, it[3], C], F32, name="zt", tag="aux", bufs=PSA)
             for b in range(it[3]):
                 nc.tensor.transpose(zt[it][:, b, :], zl[it][:, P * b : P * (b + 1)], ident[:])
 
@@ -353,17 +363,20 @@ def tile_combnethe_pa_t_kernel(tc, x_bytes, x_scale, W1o, b1o, W2o, b2o, W1f, b1
                 power_stats(o(q - 3))
                 if q - 3 == N_UNITS - 1:
                     gate_ops = gate()
-            if f(q - 3):
-                rowmin(f(q - 3))
+            if f(q - LX):
+                rowmin(f(q - LX))
             if o(q - 2):
                 exps(o(q - 2))
-            if f(q - 2):
-                logits(f(q - 2), (q - 2) % LM == LO)
-                turn_logits(f(q - 2))
-            if f(q - 3):
-                exps(f(q - 3))
-                if f(q - 3)[1] >= T1S:
-                    first_term(f(q - 3), False)
+            if f(q - LX) and EF == 1:
+                exps(f(q - LX))
+            if f(q - LG):
+                logits(f(q - LG), (q - LG) % LM == LO)
+                turn_logits(f(q - LG))
+            if f(q - LX):
+                if EF == 0:
+                    exps(f(q - LX))
+                if f(q - LX)[1] >= T1S:
+                    first_term(f(q - LX), False)
             if o(q - 1):
                 logits(o(q - 1), (q - 1) % LM == LO)
                 turn_logits(o(q - 1))
@@ -373,12 +386,13 @@ def tile_combnethe_pa_t_kernel(tc, x_bytes, x_scale, W1o, b1o, W2o, b2o, W1f, b1
             gate_ops = run_gate()
             if o(q):
                 weave(o(q))
-            if f(q - 1):
-                weave(f(q - 1))
+            if f(q - LW):
+                weave(f(q - LW))
             if q == 0:
                 nc.vector.quantize_mx(out=w2_codes[:].bitcast(FP8X4), scales=w2_scales[:], in_=w2_grp[:].rearrange("p n c j -> p (n c j)"))
+            if q == GW:
                 group_w1(1)
-            if q == 13:
+            if q == QW:
                 quant_w1(1)
             gate_ops = run_gate()
             if o(q - 1):
@@ -391,21 +405,23 @@ def tile_combnethe_pa_t_kernel(tc, x_bytes, x_scale, W1o, b1o, W2o, b2o, W1f, b1
                 return done + len(group)
 
             if q > N_UNITS + 3 and q < n_items and not gate_ops:
-                done = blend_some(done, q - 3)
+                done = blend_some(done, q - LX)
             if o(q):
                 quant_h(o(q))
                 mm2(o(q))
-            if f(q - 1):
-                quant_h(f(q - 1))
-                mm2(f(q - 1))
+            if f(q - LW):
+                quant_h(f(q - LW))
+                mm2(f(q - LW))
             gate_ops = run_gate()
             if q >= n_items:
-                done = blend_some(done, q - 2)
+                done = blend_some(done, q - LX + 1)
             gate_ops = run_gate()
-            if o(q - 2):
+            if SQ == 0 and o(q - 2):
                 squares(o(q - 2))
             if q + 2 < N_UNITS:
                 leave(q + 2, 0)
+            if SQ == 1 and o(q - 2):
+                squares(o(q - 2))
             if o(q - 2):
                 fourth_powers(o(q - 2))
             if q + 2 < N_UNITS:

@@ -24,23 +24,31 @@ BLK = UNIT // P
 N_UNITS = B // UNIT
 COLS = N_UNITS * BLK
 
-VA = 14
-VB = 23
+VA = 16
+VB = 20
 LM = 6
 LO = 2
 T1S = 8
 FILL = 2
 SPLIT = (4,)
-GW = 0
-QW = 8
+GW = 2
+PA = 10
+PB = 20
+PM = 4
+PR = 1
+LVA = 2
+LVM = 99
+EM = 99
+VM = 8
+QW = 13
 PSA = 4
 HB = 3
 ZB = 3
 LW = 0
-LG = 1
+LG = 2
 LX = 3
 SQ = 1
-EF = 1
+EF = 0
 LA = 2
 
 
@@ -62,7 +70,7 @@ def tile_combnethe_pa_t_kernel(tc, x_bytes, x_scale, W1o, b1o, W2o, b2o, W1f, b1
         w2_codes = keep.tile([P, 2 * C], U32, name="w2c", align_bytes=64)
         w2_scales = keep.tile([P, 2 * C], U8, name="w2s", align_bytes=64)
         b1 = [keep.tile([P, PACK], BF16, name="b1_%d" % n) for n in range(2)]
-        b1w = [keep.tile([P, PACK], F32, name="b1w_%d" % n) for n in range(2)]
+        b1w = [keep.tile([P, 1, PACK], F32, name="b1w_%d" % n) for n in range(2)]
         b2 = [keep.tile([P, 1], BF16, name="b2_%d" % n) for n in range(2)]
         b2n = [keep.tile([P, 1], F32, name="b2n_%d" % n) for n in range(2)]
         warm = keep.tile([P, 1], F32, name="warm")
@@ -112,7 +120,8 @@ def tile_combnethe_pa_t_kernel(tc, x_bytes, x_scale, W1o, b1o, W2o, b2o, W1f, b1
             if h == 0:
                 xg[i] = work.tile([P, UNIT, PACK], BF16, name="xg", bufs=HB, align_bytes=64)
             words = xg[i][:].rearrange("p n j -> p (n j)").bitcast(F32).rearrange("p (b r u) -> p b r u", b=BLK, u=2)
-            nc.scalar.copy(out=words[:, 2 * h : 2 * h + 2], in_=xt[i, h][:].rearrange("p b u r -> p b r u"))
+            copy = nc.vector.tensor_copy if h == 1 and i >= LVA and i % LVM == LVM - 1 else nc.scalar.copy
+            copy(out=words[:, 2 * h : 2 * h + 2], in_=xt[i, h][:].rearrange("p b u r -> p b r u"))
 
         def quant_x(i):
             codes = work.tile([P, UNIT], U32, name="xq", bufs=N_UNITS, align_bytes=64)
@@ -120,9 +129,23 @@ def tile_combnethe_pa_t_kernel(tc, x_bytes, x_scale, W1o, b1o, W2o, b2o, W1f, b1
             nc.vector.quantize_mx(out=codes[:].bitcast(FP8X4), scales=scales[:], in_=xg[i][:].rearrange("p n j -> p (n j)"))
             xq[i] = (codes, scales)
 
+        def p1(it):
+            k = N_UNITS * it[0] + it[1]
+            return PA <= k < PB and k % PM == PR and it[3] == BLK
+
         def mm1(it):
             n, i, b0, nb = it
             codes, scales = xq[i]
+            if p1(it):
+                for b in range(BLK):
+                    acc = psum.tile([P, PACK, P], F32, name="ps1", bufs=8 - PSA)
+                    tok = slice(P * b, P * (b + 1))
+                    for t in range(PACK):
+                        m = slice(P * t, P * (t + 1))
+                        nc.tensor.matmul_mx(out=acc[:, t, :], lhsT=w1_codes[n][:, m].bitcast(FP8X4), lhsT_scale=w1_scales[n][:, m],
+                                            rhs=codes[:, tok].bitcast(FP8X4), rhs_scale=scales[:, tok], start=True, stop=True)
+                    ps1[it, b] = acc
+                return
             tok = slice(P * b0, P * (b0 + nb))
             for t in range(PACK):
                 acc = psum.tile([P, P * nb], F32, name="ps1", bufs=8 - PSA)
@@ -133,14 +156,24 @@ def tile_combnethe_pa_t_kernel(tc, x_bytes, x_scale, W1o, b1o, W2o, b2o, W1f, b1
 
         def relu(it, on_vector):
             n, i, b0, nb = it
+            if p1(it):
+                hg[it] = work.tile([P, P * nb, PACK], BF16, name="hg", bufs=HB, align_bytes=64)
+                for b in range(BLK):
+                    nc.vector.tensor_tensor(out=hg[it][:, P * b : P * (b + 1), :], in0=ps1[it, b][:].rearrange("p t n -> p n t"),
+                                            in1=b1w[n][:].to_broadcast([P, P, PACK]), op=ALU.add)
+                return
             hp[it] = work.tile([P, PACK, P * nb], BF16, name="hp", bufs=HB, align_bytes=64)
             for t in range(PACK):
                 if t < PACK - on_vector:
                     nc.scalar.activation(hp[it][:, t, :], ps1[it, t][:], ACT.Relu, bias=b1[n][:, t : t + 1])
                 else:
-                    nc.vector.tensor_scalar(out=hp[it][:, t, :], in0=ps1[it, t][:], scalar1=b1w[n][:, t : t + 1], scalar2=0.0, op0=ALU.add, op1=ALU.max)
+                    nc.vector.tensor_scalar(out=hp[it][:, t, :], in0=ps1[it, t][:], scalar1=b1w[n][:, 0, t : t + 1], scalar2=0.0, op0=ALU.add, op1=ALU.max)
 
         def weave(it):
+            if p1(it):
+                flat = hg[it][:].rearrange("p n t -> p (n t)")
+                nc.vector.tensor_scalar(out=flat, in0=flat, scalar1=0.0, scalar2=None, op0=ALU.max)
+                return
             hg[it] = work.tile([P, P * it[3], PACK], BF16, name="hg", bufs=HB, align_bytes=64)
             nc.vector.tensor_copy(out=hg[it][:].rearrange("p (c i) t -> p c t i", i=4), in_=hp[it][:].rearrange("p t (c i) -> p c t i", i=4))
 
@@ -191,7 +224,10 @@ def tile_combnethe_pa_t_kernel(tc, x_bytes, x_scale, W1o, b1o, W2o, b2o, W1f, b1
 
         def fourth_powers(it):
             e4[it] = work.tile([P, it[3], C], F32, name="e4", bufs=3)
-            nc.scalar.activation(e4[it][:], e2[it][:], ACT.Square)
+            if it[1] % EM == EM - 1:
+                nc.vector.tensor_tensor(out=e4[it][:], in0=e2[it][:], in1=e2[it][:], op=ALU.mult)
+            else:
+                nc.scalar.activation(e4[it][:], e2[it][:], ACT.Square)
 
         def power_stats(it):
             n, i, b0, nb = it
@@ -323,7 +359,7 @@ def tile_combnethe_pa_t_kernel(tc, x_bytes, x_scale, W1o, b1o, W2o, b2o, W1f, b1
         widen(1, 1)
         turn(1, 1)
         for n in range(2):
-            nc.vector.tensor_copy(out=b1w[n][:], in_=b1[n][:])
+            nc.vector.tensor_copy(out=b1w[n][:, 0, :], in_=b1[n][:])
             nc.vector.tensor_scalar(out=b2n[n][:], in0=b2[n][:], scalar1=-1.0, scalar2=None, op0=ALU.mult)
         leave(1, 0)
         for n in range(2):
@@ -350,7 +386,7 @@ def tile_combnethe_pa_t_kernel(tc, x_bytes, x_scale, W1o, b1o, W2o, b2o, W1f, b1
             if 1 <= q < N_UNITS - 5:
                 load(q + 5)
             if now:
-                relu(now, 1 if VA <= q < VB else 0)
+                relu(now, 1 if VA <= q < VB or q % VM == VM - 1 else 0)
             if q == 0:
                 leave(1, 1)
             if f(q + 1):

from contextlib import ExitStack

import concourse.mybir as mybir
from concourse.masks import make_identity

B, D_IN, D_H, C = 8192, 512, 512, 128
FLOPS = 2 * (2 * B * D_IN * D_H + 2 * B * D_H * C)
TAU = 0.5

F32 = mybir.dt.float32
BF16 = mybir.dt.bfloat16
U32 = mybir.dt.uint32
U8 = mybir.dt.uint8
FP8 = mybir.dt.float8_e4m3fn
FP8X4 = mybir.dt.float8_e4m3fn_x4
ACT = mybir.ActivationFunctionType
ALU = mybir.AluOpType
AX = mybir.AxisListType

P = 128
PACK = 4
UNIT = 512
BLK = UNIT // P
N_UNITS = B // UNIT
COLS = N_UNITS * BLK

VA = 16
VB = 20
LM = 6
LO = 2
T1S = 8
FILL = 2
SPLIT = (4,)
GW = 2
PA = 10
PB = 20
PM = 4
PR = 1
LVA = 2
LVM = 99
EM = 99
VM = 8
QW = 13
PSA = 4
HB = 3
ZB = 3
LW = 0
LG = 2
LX = 3
SQ = 1
EF = 0
LA = 2


def tile_combnethe_pa_t_kernel(tc, x_bytes, x_scale, W1o, b1o, W2o, b2o, W1f, b1f, W2f, b2f, out):
    nc = tc.nc
    x_rows = x_bytes.rearrange("(i p b) k -> i p b k", p=P, b=BLK)
    out_rows = out.rearrange("(i p b) c -> i p b c", p=P, b=BLK)
    w1_in, b1_in, w2_in, b2_in = (W1o, W1f), (b1o, b1f), (W2o, W2f), (b2o, b2f)

    with ExitStack() as ctx:
        keep = ctx.enter_context(tc.tile_pool(name="keep", bufs=1))
        work = ctx.enter_context(tc.tile_pool(name="work", bufs=3))
        psum = ctx.enter_context(tc.psum_pool(name="psum", bufs=4))

        ident = keep.tile([P, P], F32, name="ident")
        scale = keep.tile([P, 2, D_IN], F32, name="scale")
        w1_codes = [keep.tile([P, D_H], U32, name="w1c%d" % n, align_bytes=64) for n in range(2)]
        w1_scales = [keep.tile([P, D_H], U8, name="w1s%d" % n, align_bytes=64) for n in range(2)]
        w2_codes = keep.tile([P, 2 * C], U32, name="w2c", align_bytes=64)
        w2_scales = keep.tile([P, 2 * C], U8, name="w2s", align_bytes=64)
        b1 = [keep.tile([P, PACK], BF16, name="b1_%d" % n) for n in range(2)]
        b1w = [keep.tile([P, 1, PACK], F32, name="b1w_%d" % n) for n in range(2)]
        b2 = [keep.tile([P, 1], BF16, name="b2_%d" % n) for n in range(2)]
        b2n = [keep.tile([P, 1], F32, name="b2n_%d" % n) for n in range(2)]
        warm = keep.tile([P, 1], F32, name="warm")
        w_raw = [keep.tile([P, PACK, D_H], BF16, name="w1raw%d" % n) for n in range(2)]
        w_grp = [keep.tile([P, D_H, PACK], BF16, name="w1grp%d" % n, align_bytes=64) for n in range(2)]
        w2_raw = keep.tile([P, 2, PACK, C], BF16, name="w2raw")
        w2_grp = keep.tile([P, 2, C, PACK], BF16, name="w2grp", align_bytes=64)
        zsum = [keep.tile([P, COLS], F32, name="zsum%d" % n) for n in range(2)]
        sum2 = keep.tile([P, COLS], F32, name="sum2")
        stats = keep.tile([P, COLS // 2, 2, 3], F32, name="stats")
        alpha = keep.tile([P, COLS], F32, name="alpha")
        cond = keep.tile([P, COLS], F32, name="cond")

        xb, xs, xt, xg, xq = {}, {}, {}, {}, {}
        ps1, hp, hg, hq, ps2, zl, zt, nm, ez, e2, e4, t1 = {}, {}, {}, {}, {}, {}, {}, {}, {}, {}, {}, {}

        def load(i):
            xb[i] = work.tile([P, BLK, D_IN], U8, name="xb", bufs=6)
            nc.sync.dma_start(out=xb[i][:], in_=x_rows[i])

        def load_w1(n):
            nc.sync.dma_start(out=w_raw[n][:], in_=w1_in[n].rearrange("(p j) c -> p j c", j=PACK))

        def group_w1(n):
            nc.scalar.copy(out=w_grp[n][:].rearrange("p (t m) j -> p t m j", t=PACK), in_=w_raw[n][:].rearrange("p j (m t) -> p t m j", t=PACK))

        def quant_w1(n):
            nc.vector.quantize_mx(out=w1_codes[n][:].bitcast(FP8X4), scales=w1_scales[n][:], in_=w_grp[n][:].rearrange("p c j -> p (c j)"))

        def widen(i, h):
            xs[i, h] = work.tile([P, 2, D_IN], BF16, name="xs", bufs=4, align_bytes=64)
            nc.vector.tensor_tensor(
                out=xs[i, h][:].rearrange("p b k -> p (b k)"),
                in0=xb[i][:, 2 * h : 2 * h + 2, :].rearrange("p b k -> p (b k)").bitcast(FP8),
                in1=scale[:].rearrange("p b k -> p (b k)"),
                op=ALU.mult,
            )

        def turn(i, h):
            xt[i, h] = psum.tile([P, 2, 2, P], F32, name="xt", tag="aux", bufs=PSA)
            words = xs[i, h][:].rearrange("p b k -> p (b k)").bitcast(F32)
            for b in range(2):
                for u in range(2):
                    nc.tensor.transpose(xt[i, h][:, b, u, :], words[:, 256 * b + u : 256 * (b + 1) : 2], ident[:])

        def leave(i, h):
            if h == 0:
                xg[i] = work.tile([P, UNIT, PACK], BF16, name="xg", bufs=HB, align_bytes=64)
            words = xg[i][:].rearrange("p n j -> p (n j)").bitcast(F32).rearrange("p (b r u) -> p b r u", b=BLK, u=2)
            copy = nc.vector.tensor_copy if h == 1 and i >= LVA and i % LVM == LVM - 1 else nc.scalar.copy
            copy(out=words[:, 2 * h : 2 * h + 2], in_=xt[i, h][:].rearrange("p b u r -> p b r u"))

        def quant_x(i):
            codes = work.tile([P, UNIT], U32, name="xq", bufs=N_UNITS, align_bytes=64)
            scales = work.tile([P, UNIT], U8, name="xqs", bufs=N_UNITS, align_bytes=64)
            nc.vector.quantize_mx(out=codes[:].bitcast(FP8X4), scales=scales[:], in_=xg[i][:].rearrange("p n j -> p (n j)"))
            xq[i] = (codes, scales)

        def p1(it):
            k = N_UNITS * it[0] + it[1]
            return PA <= k < PB and k % PM == PR and it[3] == BLK

        def mm1(it):
            n, i, b0, nb = it
            codes, scales = xq[i]
            if p1(it):
                for b in range(BLK):
                    acc = psum.tile([P, PACK, P], F32, name="ps1", bufs=8 - PSA)
                    tok = slice(P * b, P * (b + 1))
                    for t in range(PACK):
                        m = slice(P * t, P * (t + 1))
                        nc.tensor.matmul_mx(out=acc[:, t, :], lhsT=w1_codes[n][:, m].bitcast(FP8X4), lhsT_scale=w1_scales[n][:, m],
                                            rhs=codes[:, tok].bitcast(FP8X4), rhs_scale=scales[:, tok], start=True, stop=True)
                    ps1[it, b] = acc
                return
            tok = slice(P * b0, P * (b0 + nb))
            for t in range(PACK):
                acc = psum.tile([P, P * nb], F32, name="ps1", bufs=8 - PSA)
                m = slice(P * t, P * (t + 1))
                nc.tensor.matmul_mx(out=acc[:], lhsT=w1_codes[n][:, m].bitcast(FP8X4), lhsT_scale=w1_scales[n][:, m],
                                    rhs=codes[:, tok].bitcast(FP8X4), rhs_scale=scales[:, tok], start=True, stop=True)
                ps1[it, t] = acc

        def relu(it, on_vector):
            n, i, b0, nb = it
            if p1(it):
                hg[it] = work.tile([P, P * nb, PACK], BF16, name="hg", bufs=HB, align_bytes=64)
                for b in range(BLK):
                    nc.vector.tensor_tensor(out=hg[it][:, P * b : P * (b + 1), :], in0=ps1[it, b][:].rearrange("p t n -> p n t"),
                                            in1=b1w[n][:].to_broadcast([P, P, PACK]), op=ALU.add)
                return
            hp[it] = work.tile([P, PACK, P * nb], BF16, name="hp", bufs=HB, align_bytes=64)
            for t in range(PACK):
                if t < PACK - on_vector:
                    nc.scalar.activation(hp[it][:, t, :], ps1[it, t][:], ACT.Relu, bias=b1[n][:, t : t + 1])
                else:
                    nc.vector.tensor_scalar(out=hp[it][:, t, :], in0=ps1[it, t][:], scalar1=b1w[n][:, 0, t : t + 1], scalar2=0.0, op0=ALU.add, op1=ALU.max)

        def weave(it):
            if p1(it):
                flat = hg[it][:].rearrange("p n t -> p (n t)")
                nc.vector.tensor_scalar(out=flat, in0=flat, scalar1=0.0, scalar2=None, op0=ALU.max)
                return
            hg[it] = work.tile([P, P * it[3], PACK], BF16, name="hg", bufs=HB, align_bytes=64)
            nc.vector.tensor_copy(out=hg[it][:].rearrange("p (c i) t -> p c t i", i=4), in_=hp[it][:].rearrange("p t (c i) -> p c t i", i=4))

        def quant_h(it):
            codes = work.tile([P, P * it[3]], U32, name="hq", bufs=3, align_bytes=64)
            scales = work.tile([P, P * it[3]], U8, name="hqs", bufs=3, align_bytes=64)
            nc.vector.quantize_mx(out=codes[:].bitcast(FP8X4), scales=scales[:], in_=hg[it][:].rearrange("p n j -> p (n j)"))
            hq[it] = (codes, scales)

        def mm2(it):
            n, i, b0, nb = it
            codes, scales = hq[it]
            ps2[it] = psum.tile([P, P * nb], F32, name="ps2", tag="aux", bufs=PSA)
            w = slice(C * n, C * (n + 1))
            nc.tensor.matmul_mx(out=ps2[it][:], lhsT=w2_codes[:, w].bitcast(FP8X4), lhsT_scale=w2_scales[:, w],
                                rhs=codes[:].bitcast(FP8X4), rhs_scale=scales[:], start=True, stop=True)

        def logits(it, on_vector):
            n, i, b0, nb = it
            zl[it] = work.tile([P, P * nb], F32, name="zl", bufs=ZB)
            if on_vector:
                nc.vector.tensor_scalar(out=zl[it][:], in0=ps2[it][:], scalar1=-1.0, scalar2=b2n[n][:], op0=ALU.mult, op1=ALU.add)
            else:
                nc.scalar.activation(zl[it][:], ps2[it][:], ACT.Identity, bias=b2n[n][:], scale=-1.0)

        def turn_logits(it):
            zt[it] = psum.tile([P, it[3], C], F32, name="zt", tag="aux", bufs=PSA)
            for b in range(it[3]):
                nc.tensor.transpose(zt[it][:, b, :], zl[it][:, P * b : P * (b + 1)], ident[:])

        def rowmin(it):
            nm[it] = work.tile([P, it[3]], F32, name="nm", bufs=4)
            nc.vector.tensor_reduce(out=nm[it][:], in_=zt[it][:], axis=AX.X, op=ALU.min)

        def exps(it):
            n, i, b0, nb = it
            ez[it] = work.tile([P, nb, C], F32, name="ez%d" % n, bufs=N_UNITS if n == 0 else 9)
            for b in range(nb):
                c = BLK * i + b0 + b
                nc.scalar.activation(ez[it][:, b, :], zt[it][:, b, :], ACT.Exp, bias=nm[it][:, b : b + 1], scale=-1.0, accum_out=zsum[n][:, c : c + 1])

        def squares(it):
            n, i, b0, nb = it
            e2[it] = work.tile([P, nb, C], F32, name="e2", bufs=2)
            for b in range(nb):
                c = BLK * i + b0 + b
                nc.scalar.activation(e2[it][:, b, :], ez[it][:, b, :], ACT.Square, accum_out=sum2[:, c : c + 1])

        def fourth_powers(it):
            e4[it] = work.tile([P, it[3], C], F32, name="e4", bufs=3)
            if it[1] % EM == EM - 1:
                nc.vector.tensor_tensor(out=e4[it][:], in0=e2[it][:], in1=e2[it][:], op=ALU.mult)
            else:
                nc.scalar.activation(e4[it][:], e2[it][:], ACT.Square)

        def power_stats(it):
            n, i, b0, nb = it
            for h in range(0, nb, 2):
                nc.vector.bn_stats(out=stats[:, (BLK * i + b0 + h) // 2].rearrange("p b s -> p (b s)"), in_=e4[it][:, h : h + 2, :].rearrange("p b c -> p c b"))

        def gate():
            t = {"z": zsum[0], "s2": sum2, "cond": cond, "alpha": alpha}
            ops = []
            per = stats[:].rearrange("p g b s -> p (g b) s")
            mean, m2 = per[:, :, 1], per[:, :, 2]

            def new(key):
                if key not in t:
                    t[key] = work.tile([P, COLS], F32, name="g_" + key, bufs=1)
                return t[key][:]

            def val(a):
                return t[a][:] if isinstance(a, str) else a

            def recip(dst, a):
                ops.append(lambda: nc.vector.reciprocal(out=new(dst), in_=val(a)))

            def mul(dst, a, b):
                ops.append(lambda: nc.vector.tensor_tensor(out=new(dst), in0=val(a), in1=val(b), op=ALU.mult))

            def lin(dst, a, m, c):
                ops.append(lambda: nc.vector.tensor_scalar(out=new(dst), in0=val(a), scalar1=m, scalar2=c, op0=ALU.mult, op1=ALU.add))

            def fma(dst, a, op0, s, op1, b):
                ops.append(lambda: nc.vector.scalar_tensor_tensor(out=new(dst), in0=val(a), scalar=s, in1=val(b), op0=op0, op1=op1))

            def inv(r, v, vm, vc, two_over_m, extra):
                lin("y" + r, v, vm, vc)
                lin("a" + r, v, vm * two_over_m, (vc + 1.0) * two_over_m)
                mul("y2" + r, "y" + r, "y" + r)
                extra()
                mul("y4" + r, "y2" + r, "y2" + r)
                fma("b" + r, "y2" + r, ALU.add, 1.0, ALU.mult, "a" + r)
                mul("y8" + r, "y4" + r, "y4" + r)
                fma("c" + r, "y4" + r, ALU.add, 1.0, ALU.mult, "b" + r)
                fma("d" + r, "y8" + r, ALU.add, 1.0, ALU.mult, "c" + r)
                return "d" + r

            n = float(C)
            t2, t4, t8 = TAU**2, TAU**4, TAU**8
            m0 = 2.0 + t2
            recip("r", "z")
            mul("msq", mean, mean)
            mul("q", "r", "r")
            fma("s8", "msq", ALU.mult, n, ALU.add, m2)
            mul("u1", "s2", "q")
            mul("q2", "q", "q")
            k1 = inv("i", "u1", -2.0 / m0, 1.0 - 2.0 / m0 * t2, 2.0 / m0, lambda: fma("u2", mean, ALU.mult, n, ALU.mult, "q2"))
            mul("q4", "q2", "q2")
            mul("k1s", k1, k1)
            mul("u3", "s8", "q4")
            fma("v2", "u2", ALU.add, t4, ALU.mult, "k1s")
            i2 = inv("j", "v2", -1.0, 1.0, 1.0, lambda: lin("nr", "r", -1.0, 0.0))
            mul("k2", "k1s", i2)
            mul("k2s", "k2", "k2")
            fma("v3", "u3", ALU.add, t8, ALU.mult, "k2s")
            i3 = inv("k", "v3", -1.0, 1.0, 1.0, lambda: lin("k2t", "k2s", t8, 0.0))
            mul("cond", "k2t", i3)
            fma("alpha", "cond", ALU.subtract, 1.0, ALU.mult, "nr")
            return ops

        def first_term(it, on_vector):
            n, i, b0, nb = it
            t1[it] = work.tile([P, nb, C], F32, name="t1", bufs=5)
            for b in range(nb):
                a = alpha[:, BLK * i + b0 + b : BLK * i + b0 + b + 1]
                if on_vector:
                    nc.vector.tensor_scalar(out=t1[it][:, b, :], in0=ez[0, i, 0, BLK][:, b0 + b, :], scalar1=a, scalar2=None, op0=ALU.mult)
                else:
                    nc.scalar.activation(t1[it][:, b, :], ez[0, i, 0, BLK][:, b0 + b, :], ACT.Copy, scale=a)

        def blend(group):
            c0 = BLK * group[0][1] + group[0][2]
            c1 = BLK * group[-1][1] + group[-1][2] + group[-1][3]
            rz = work.tile([P, c1 - c0], F32, name="rz", bufs=2)
            beta = work.tile([P, c1 - c0], F32, name="beta", bufs=2)
            nc.vector.reciprocal(out=rz[:], in_=zsum[1][:, c0:c1])
            todo = [it for it in group if it not in t1]
            for it in todo:
                first_term(it, True)
            nc.vector.tensor_tensor(out=beta[:], in0=rz[:], in1=cond[:, c0:c1], op=ALU.mult)
            for it in group:
                n, i, b0, nb = it
                ob = work.tile([P, nb, C], F32, name="ob", bufs=4)
                for b in range(nb):
                    c = BLK * i + b0 + b - c0
                    nc.vector.scalar_tensor_tensor(out=ob[:, b, :], in0=ez[it][:, b, :], scalar=beta[:, c : c + 1], in1=t1[it][:, b, :], op0=ALU.mult, op1=ALU.add)
                nc.sync.dma_start(out=out_rows[i][:, b0 : b0 + nb, :], in_=ob[:])

        nc.vector.memset(warm[:], 0.0)
        make_identity(nc, ident[:])
        nc.sync.dma_start(out=scale[:, 0, :], in_=x_scale.rearrange("o k -> (o k)").partition_broadcast(P))
        load(0)
        load_w1(0)
        load(1)
        for n in range(2):
            nc.sync.dma_start(out=w2_raw[:, n], in_=w2_in[n].rearrange("(p j) c -> p j c", j=PACK))
        load(2)
        load_w1(1)
        for n in range(2):
            nc.scalar.dma_start(out=b1[n][:], in_=b1_in[n].rearrange("(p t) -> p t", t=PACK))
            nc.scalar.dma_start(out=b2[n][:], in_=b2_in[n].rearrange("(c o) -> c o", o=1))
        for i in range(3, 6):
            load(i)
        nc.scalar.activation(warm[:], warm[:], ACT.Exp)
        group_w1(0)
        nc.vector.tensor_copy(out=scale[:, 1, :], in_=scale[:, 0, :])
        for h in range(2):
            widen(0, h)
            turn(0, h)
            leave(0, h)
        widen(1, 0)
        turn(1, 0)
        quant_w1(0)
        quant_x(0)

        items = [(0, i, 0, BLK) for i in range(N_UNITS)] + [(1, i, 0, BLK) for i in range(N_UNITS - 1)]
        b0 = 0
        for nb in SPLIT:
            items.append((1, N_UNITS - 1, b0, nb))
            b0 += nb
        mm1(items[0])
        widen(1, 1)
        turn(1, 1)
        for n in range(2):
            nc.vector.tensor_copy(out=b1w[n][:, 0, :], in_=b1[n][:])
            nc.vector.tensor_scalar(out=b2n[n][:], in0=b2[n][:], scalar1=-1.0, scalar2=None, op0=ALU.mult)
        leave(1, 0)
        for n in range(2):
            nc.scalar.copy(out=w2_grp[:, n], in_=w2_raw[:, n].rearrange("p j c -> p c j"))

        n_items = len(items)
        gate_ops = []
        done = N_UNITS

        def run_gate():
            for op in gate_ops[:FILL]:
                op()
            return gate_ops[FILL:]

        for q in range(n_items + 4):

            def o(k):
                return items[k] if 0 <= k < N_UNITS else None

            def f(k):
                return items[k] if N_UNITS <= k < n_items else None

            now, nxt = o(q) or f(q), o(q + 1) or f(q + 1)
            if 1 <= q < N_UNITS - 5:
                load(q + 5)
            if now:
                relu(now, 1 if VA <= q < VB or q % VM == VM - 1 else 0)
            if q == 0:
                leave(1, 1)
            if f(q + 1):
                mm1(nxt)
            if q + 2 < N_UNITS:
                for h in range(2):
                    widen(q + 2, h)
                    turn(q + 2, h)
            if o(q - 3):
                power_stats(o(q - 3))
                if q - 3 == N_UNITS - 1:
                    gate_ops = gate()
            if f(q - LX):
                rowmin(f(q - LX))
            if o(q - 2):
                exps(o(q - 2))
            if f(q - LX) and EF == 1:
                exps(f(q - LX))
            if f(q - LG):
                logits(f(q - LG), (q - LG) % LM == LO)
                turn_logits(f(q - LG))
            if f(q - LX):
                if EF == 0:
                    exps(f(q - LX))
                if f(q - LX)[1] >= T1S:
                    first_term(f(q - LX), False)
            if o(q - 1):
                logits(o(q - 1), (q - 1) % LM == LO)
                turn_logits(o(q - 1))
            if o(q + 1):
                quant_x(q + 1)
                mm1(nxt)
            gate_ops = run_gate()
            if o(q):
                weave(o(q))
            if f(q - LW):
                weave(f(q - LW))
            if q == 0:
                nc.vector.quantize_mx(out=w2_codes[:].bitcast(FP8X4), scales=w2_scales[:], in_=w2_grp[:].rearrange("p n c j -> p (n c j)"))
            if q == GW:
                group_w1(1)
            if q == QW:
                quant_w1(1)
            gate_ops = run_gate()
            if o(q - 1):
                rowmin(o(q - 1))

            def blend_some(done, upto):
                group = items[done : max(done, min(upto, done + 2))]
                if group:
                    blend(group)
                return done + len(group)

            if q > N_UNITS + 3 and q < n_items and not gate_ops:
                done = blend_some(done, q - LX)
            if o(q):
                quant_h(o(q))
                mm2(o(q))
            if f(q - LW):
                quant_h(f(q - LW))
                mm2(f(q - LW))
            gate_ops = run_gate()
            if q >= n_items:
                done = blend_some(done, q - LX + 1)
            gate_ops = run_gate()
            if SQ == 0 and o(q - 2):
                squares(o(q - 2))
            if q + 2 < N_UNITS:
                leave(q + 2, 0)
            if SQ == 1 and o(q - 2):
                squares(o(q - 2))
            if o(q - 2):
                fourth_powers(o(q - 2))
            if q + 2 < N_UNITS:
                leave(q + 2, 1)
        assert done == n_items
